import numpy as np
import ml_dtypes


def mxq(x, axis, fmt="e4m3"):
    dtype, down = {"e4m3": (ml_dtypes.float8_e4m3fn, 7), "e5m2": (ml_dtypes.float8_e5m2, 14)}[fmt]
    v = np.moveaxis(np.asarray(x, np.float32).astype(ml_dtypes.bfloat16).astype(np.float64), axis, -1)
    blocks = v.reshape(v.shape[:-1] + (-1, 32))
    amax = np.abs(blocks).max(-1, keepdims=True)
    byte = np.maximum(np.where(amax > 0, np.frexp(amax)[1] - 1 + 127, 0) - down, 1)
    scale = np.exp2(byte - 127.0)
    codes = (blocks / scale).astype(np.float32).astype(dtype).astype(np.float64)
    return np.moveaxis((codes * scale).reshape(v.shape), -1, axis)


WIDE = False


def mx_kscale(k):
    if not WIDE:
        return np.ones(k)
    levels = np.array([10, -10, 5, -5, 0])
    a = np.random.permutation(np.resize(levels, k // 512 * 4)).reshape(k // 512, 4)
    idx = np.arange(k)
    return np.exp2(a[idx // 512, idx % 128 // 32])


BF16 = ml_dtypes.bfloat16


def bf(x):
    return np.asarray(x, np.float32).astype(BF16)


def f64(x):
    return np.asarray(x).astype(np.float64)


B, DIN, H1, H2, N, I, K, O = 4096, 2048, 1024, 1024, 32, 8, 256, 16
NI = N * I
LN_EPS = 1e-5


def setup_inputs():
    s, t = mx_kscale(H1), mx_kscale(H2)
    return {"h1": bf(np.maximum(np.random.standard_normal((B, H1)), 0.0) * s),
            "W2": bf(np.random.standard_normal((H1, H2)) * 1.4 / np.sqrt(H1) / s[:, None] * t),
            "b2": bf(np.random.standard_normal(H2) * 0.2 * t),
            "Wp": bf(np.random.standard_normal((N, H2, I)) * 1.4 / np.sqrt(H2) / t[None, :, None]),
            "bp": bf(np.random.standard_normal((N, I)) * 0.2),
            "ln_g": bf(1.0 + 0.1 * np.random.standard_normal((N, I))),
            "ln_b": bf(0.1 * np.random.standard_normal((N, I)))}


def reference(h1, W2, b2, Wp, bp, ln_g, ln_b):
    x = np.maximum((mxq(f64(h1), 1, "e4m3") @ mxq(f64(W2), 0, "e4m3")) + f64(b2), 0.0)
    wpf = f64(Wp).transpose(1, 0, 2).reshape(H2, NI)
    p = (mxq(x, 1, "e4m3") @ mxq(wpf, 0, "e4m3")).reshape(B, N, I) + f64(bp)
    mu = p.mean(-1, keepdims=True)
    var = ((p - mu) ** 2).mean(-1, keepdims=True)
    return (p - mu) / np.sqrt(var + LN_EPS) * f64(ln_g) + f64(ln_b)

@@ -1,0 +1,320 @@
+from contextlib import ExitStack
+
+import concourse.mybir as mybir
+from concourse.masks import make_identity
+
+F32 = mybir.dt.float32
+BF16 = mybir.dt.bfloat16
+U32 = mybir.dt.uint32
+U8 = mybir.dt.uint8
+FP8X4 = mybir.dt.float8_e4m3fn_x4
+ALU = mybir.AluOpType
+ACT = mybir.ActivationFunctionType
+AXIS = mybir.AxisListType
+
+P = 128
+PACK = 4
+K_PASS = P * PACK
+BATCH, H1, H2, CAPS, CAP_DIM = 4096, 1024, 1024, 32, 8
+NI = CAPS * CAP_DIM
+PASSES = H1 // K_PASS
+CHUNK = 512
+SUB = CHUNK // P
+N_CHUNKS = BATCH // CHUNK
+M_TILES = H2 // P
+NI_TILES = NI // P
+LN_EPS = 1e-5
+
+FLOPS = 2 * BATCH * H1 * H2 + 2 * BATCH * H2 * NI
+
+
+def tile_capsulenetwork_pa_t_kernel(tc, h1, W2, b2, Wp, bp, ln_g, ln_b, out):
+    nc = tc.nc
+    out_rows = out.rearrange("b n i -> b (n i)")
+
+    with ExitStack() as ctx:
+        consts = ctx.enter_context(tc.tile_pool(name="consts", bufs=1))
+        weights = ctx.enter_context(tc.tile_pool(name="weights", bufs=1))
+        wstage = ctx.enter_context(tc.tile_pool(name="wstage", bufs=2))
+        hpool = ctx.enter_context(tc.tile_pool(name="hpool", bufs=3))
+        xpool = ctx.enter_context(tc.tile_pool(name="xpool", bufs=2))
+        lnpool = ctx.enter_context(tc.tile_pool(name="lnpool", bufs=2))
+        psum = ctx.enter_context(tc.psum_pool(name="psum", bufs=8))
+        ctx.enter_context(tc.manual_schedule())
+
+        h_raw_tiles = {}
+        h_mx = {}
+        x_mx = {}
+        u_tiles = {}
+        centred = {}
+        sum_sq_tiles = {}
+        rstd_tiles = {}
+
+        def load_h1(c):
+            h_raw = hpool.tile([P, SUB * H1], BF16, name="h_raw")
+            nc.sync.dma_start(
+                out=h_raw[:],
+                in_=h1[c * CHUNK : (c + 1) * CHUNK, :].rearrange("(p s) k -> p (s k)", s=SUB),
+            )
+            h_raw_tiles[c] = h_raw
+
+        b2_bf = consts.tile([P, PASSES, PACK], BF16)
+        nc.scalar.dma_start(out=b2_bf[:], in_=b2.rearrange("(g p t) -> p g t", g=PASSES, t=PACK))
+        bp_bf = consts.tile([P, NI_TILES], BF16)
+        with nc.allow_non_contiguous_dma(reason="256 bias values, one to a partition"):
+            nc.scalar.dma_start(
+                out=bp_bf[:], in_=bp.rearrange("n i -> (n i)").rearrange("(j q) -> q j", j=NI_TILES)
+            )
+
+        w2_raw = weights.tile([P, PASSES * PACK, H2], BF16)
+
+        def load_w2(half):
+            cols = slice(half * K_PASS, (half + 1) * K_PASS)
+            for a in range(PASSES * 2):
+                nc.sync.dma_start(
+                    out=w2_raw[:, 2 * a : 2 * a + 2, cols],
+                    in_=W2[a * 256 : (a + 1) * 256, cols].rearrange("(q e) c -> q e c", e=2),
+                )
+
+        load_w2(0)
+        load_h1(0)
+        load_w2(1)
+        load_h1(1)
+        wp_raw = weights.tile([P, PASSES, CAPS, PACK * CAP_DIM], BF16)
+        for g in range(PASSES):
+            nc.sync.dma_start(
+                out=wp_raw[:, g, :, :],
+                in_=Wp[:, g * K_PASS : (g + 1) * K_PASS, :].rearrange("n (p t) i -> p n (t i)", t=PACK),
+            )
+        load_h1(2)
+        gain = consts.tile([P, NI], BF16)
+        nc.sync.dma_start(out=gain[:], in_=ln_g.rearrange("n i -> (n i)").partition_broadcast(P))
+        shift = consts.tile([P, NI], BF16)
+        nc.sync.dma_start(out=shift[:], in_=ln_b.rearrange("n i -> (n i)").partition_broadcast(P))
+
+        eps = consts.tile([P, 1], F32)
+        nc.vector.memset(eps[:], LN_EPS)
+        warm = consts.tile([P, 1], F32)
+        nc.scalar.activation(out=warm[:], in_=eps[:], func=ACT.Abs_reciprocal_sqrt)
+        ident = consts.tile([P, P], F32)
+        make_identity(nc, ident[:])
+        in_group = consts.tile([P, P // CAP_DIM], F32)
+        nc.vector.tensor_reduce(
+            out=in_group[:], in_=ident[:].rearrange("p (n i) -> p n i", i=CAP_DIM), axis=AXIS.X, op=ALU.add
+        )
+        centre = consts.tile([P, P], F32)
+        nc.vector.scalar_tensor_tensor(
+            out=centre[:].rearrange("p (n i) -> p n i", i=CAP_DIM),
+            in0=in_group[:].unsqueeze(2).to_broadcast([P, P // CAP_DIM, CAP_DIM]),
+            scalar=-1.0 / CAP_DIM,
+            in1=ident[:].rearrange("p (n i) -> p n i", i=CAP_DIM),
+            op0=ALU.mult,
+            op1=ALU.add,
+        )
+        b2_f = consts.tile([P, M_TILES], F32)
+        nc.vector.tensor_copy(out=b2_f[:], in_=b2_bf[:].rearrange("p g t -> p (g t)"))
+        bp_f = consts.tile([P, NI_TILES], F32)
+        nc.vector.tensor_copy(out=bp_f[:], in_=bp_bf[:])
+
+        w2_codes = weights.tile([P, PASSES, H2], U32, align_bytes=64)
+        w2_scales = weights.tile([P, PASSES, H2], U8, align_bytes=64)
+
+        def quantise_w2(half):
+            cols = slice(half * K_PASS, (half + 1) * K_PASS)
+            grouped = []
+            for g in range(PASSES):
+                w2_grp = wstage.tile([P, K_PASS, PACK], BF16, align_bytes=64)
+                nc.vector.tensor_copy(
+                    out=w2_grp[:].rearrange("p (t q) j -> p t q j", t=PACK),
+                    in_=w2_raw[:, PACK * g : PACK * (g + 1), cols].rearrange("p j (q t) -> p t q j", t=PACK),
+                )
+                grouped.append(w2_grp)
+            for g in range(PASSES):
+                nc.vector.quantize_mx(
+                    out=w2_codes[:, g, cols].bitcast(FP8X4),
+                    scales=w2_scales[:, g, cols],
+                    in_=grouped[g][:].rearrange("p c j -> p (c j)"),
+                )
+
+        wp_codes = weights.tile([P, PASSES, NI], U32, align_bytes=64)
+        wp_scales = weights.tile([P, PASSES, NI], U8, align_bytes=64)
+
+        def quantise_wp():
+            grouped = []
+            for g in range(PASSES):
+                wp_grp = wstage.tile([P, NI, PACK], BF16, align_bytes=64)
+                nc.vector.tensor_copy(
+                    out=wp_grp[:].rearrange("p (n i) t -> p n i t", i=CAP_DIM),
+                    in_=wp_raw[:, g, :, :].rearrange("p n (t i) -> p n i t", t=PACK),
+                )
+                grouped.append(wp_grp)
+            for g in range(PASSES):
+                nc.vector.quantize_mx(
+                    out=wp_codes[:, g, :].bitcast(FP8X4),
+                    scales=wp_scales[:, g, :],
+                    in_=grouped[g][:].rearrange("p c t -> p (c t)"),
+                )
+
+        def transposes(c):
+            h_words = h_raw_tiles.pop(c)[:].bitcast(F32)
+            h_codes = hpool.tile([P, PASSES, CHUNK], U32, align_bytes=64)
+            h_scales = hpool.tile([P, PASSES, CHUNK], U8, align_bytes=64)
+            for g in range(PASSES):
+                h_grp = hpool.tile([P, CHUNK * PACK], BF16, align_bytes=64)
+                h_grp_words = h_grp[:].bitcast(F32).rearrange("p (b u) -> p b u", u=2)
+                for hf in range(2):
+                    tr = psum.tile([P, 2, 2 * P], F32, tag="bank")
+                    for u in range(2):
+                        for sl in range(2):
+                            first = (2 * hf + sl) * (H1 // 2) + 256 * g + P * u
+                            nc.tensor.transpose(
+                                tr[:, u, sl * P : (sl + 1) * P], h_words[:, first : first + P], ident[:]
+                            )
+                    nc.scalar.copy(
+                        out=h_grp_words[:, hf * 2 * P : (hf + 1) * 2 * P, :], in_=tr[:].rearrange("p u b -> p b u")
+                    )
+                nc.vector.quantize_mx(
+                    out=h_codes[:, g, :].bitcast(FP8X4), scales=h_scales[:, g, :], in_=h_grp[:]
+                )
+            h_mx[c] = (h_codes, h_scales)
+
+        def stage1(c):
+            h_codes, h_scales = h_mx.pop(c)
+            x_codes = xpool.tile([P, PASSES, CHUNK], U32, align_bytes=64)
+            x_scales = xpool.tile([P, PASSES, CHUNK], U8, align_bytes=64)
+            for g2 in range(PASSES):
+                x_rows = xpool.tile([P, PACK, CHUNK], BF16)
+                for t in range(PACK):
+                    m = PACK * g2 + t
+                    acc = psum.tile([P, CHUNK], F32, tag="bank")
+                    for g in range(PASSES):
+                        nc.tensor.matmul_mx(
+                            out=acc[:],
+                            lhsT=w2_codes[:, g, m * P : (m + 1) * P].bitcast(FP8X4),
+                            lhsT_scale=w2_scales[:, g, m * P : (m + 1) * P],
+                            rhs=h_codes[:, g, :].bitcast(FP8X4),
+                            rhs_scale=h_scales[:, g, :],
+                            start=(g == 0),
+                            stop=(g == PASSES - 1),
+                        )
+                    nc.scalar.activation(
+                        out=x_rows[:, t, :], in_=acc[:], func=ACT.Relu, bias=b2_f[:, m : m + 1], scale=1.0
+                    )
+                x_grp = xpool.tile([P, CHUNK, PACK], BF16, align_bytes=64)
+                nc.vector.tensor_copy(
+                    out=x_grp[:].rearrange("p (c i) t -> p c t i", i=4),
+                    in_=x_rows[:].rearrange("p t (c i) -> p c t i", i=4),
+                )
+                nc.vector.quantize_mx(
+                    out=x_codes[:, g2, :].bitcast(FP8X4),
+                    scales=x_scales[:, g2, :],
+                    in_=x_grp[:].rearrange("p b t -> p (b t)"),
+                )
+            x_mx[c] = (x_codes, x_scales)
+
+        def stage2_block(c, j):
+            x_codes, x_scales = x_mx[c]
+            acc2 = psum.tile([P, CHUNK], F32, tag="bank")
+            for g2 in range(PASSES):
+                nc.tensor.matmul_mx(
+                    out=acc2[:],
+                    lhsT=wp_codes[:, g2, j * P : (j + 1) * P].bitcast(FP8X4),
+                    lhsT_scale=wp_scales[:, g2, j * P : (j + 1) * P],
+                    rhs=x_codes[:, g2, :].bitcast(FP8X4),
+                    rhs_scale=x_scales[:, g2, :],
+                    start=(g2 == 0),
+                    stop=(g2 == PASSES - 1),
+                )
+            nc.scalar.activation(
+                out=u_tiles[c][:, j, :], in_=acc2[:], func=ACT.Identity, bias=bp_f[:, j : j + 1], scale=1.0
+            )
+
+        GROUPS = 2 * CAPS
+
+        def centre_and_square(c):
+            u_sb = u_tiles.pop(c)
+            sum_sq = lnpool.tile([P, 2 * GROUPS], F32)
+            centred[c] = []
+            for hf in range(2):
+                cb = psum.tile([P, 2, NI], F32, tag="bank")
+                for sl in range(2):
+                    s = 2 * hf + sl
+                    for j in range(NI_TILES):
+                        nc.tensor.matmul(
+                            out=cb[:, sl, j * P : (j + 1) * P],
+                            lhsT=u_sb[:, j, s * P : (s + 1) * P],
+                            rhs=centre[:],
+                            start=True,
+                            stop=True,
+                        )
+                sq = lnpool.tile([P, 2 * NI], F32)
+                nc.scalar.activation(out=sq[:], in_=cb[:].rearrange("p s f -> p (s f)"), func=ACT.Square)
+                nc.vector.tensor_reduce(
+                    out=sum_sq[:, hf * GROUPS : (hf + 1) * GROUPS],
+                    in_=sq[:].rearrange("p (n i) -> p n i", i=CAP_DIM),
+                    axis=AXIS.X,
+                    op=ALU.add,
+                )
+                centred[c].append(cb)
+            sum_sq_tiles[c] = sum_sq
+
+        def inverse_std(c):
+            rstd = lnpool.tile([P, 2 * GROUPS], F32)
+            nc.scalar.activation(
+                out=rstd[:], in_=sum_sq_tiles.pop(c)[:], func=ACT.Abs_reciprocal_sqrt, bias=eps[:], scale=1.0 / CAP_DIM
+            )
+            rstd_tiles[c] = rstd
+
+        def finish_layernorm(c):
+            rstd = rstd_tiles.pop(c)
+            banks = centred.pop(c)
+            y = lnpool.tile([P, SUB, NI], F32, bufs=3)
+            for hf in range(2):
+                nc.vector.tensor_tensor(
+                    out=y[:, 2 * hf : 2 * hf + 2, :].rearrange("p s (n i) -> p (s n) i", i=CAP_DIM),
+                    in0=banks[hf][:].rearrange("p s (n i) -> p (s n) i", i=CAP_DIM),
+                    in1=rstd[:, hf * GROUPS : (hf + 1) * GROUPS].unsqueeze(2).to_broadcast([P, GROUPS, CAP_DIM]),
+                    op=ALU.mult,
+                )
+            for hf in range(2):
+                nc.vector.tensor_tensor(
+                    out=y[:, 2 * hf : 2 * hf + 2, :],
+                    in0=y[:, 2 * hf : 2 * hf + 2, :],
+                    in1=gain[:].unsqueeze(1).to_broadcast([P, 2, NI]),
+                    op=ALU.mult,
+                )
+            for hf in range(2):
+                nc.vector.tensor_tensor(
+                    out=y[:, 2 * hf : 2 * hf + 2, :],
+                    in0=y[:, 2 * hf : 2 * hf + 2, :],
+                    in1=shift[:].unsqueeze(1).to_broadcast([P, 2, NI]),
+                    op=ALU.add,
+                )
+            nc.sync.dma_start(
+                out=out_rows[c * CHUNK : (c + 1) * CHUNK, :].rearrange("(p s) f -> p s f", s=SUB), in_=y[:]
+            )
+
+        quantise_w2(0)
+        transposes(0)
+        quantise_w2(1)
+        quantise_wp()
+        for c in range(N_CHUNKS + 2):
+            if c + 3 < N_CHUNKS:
+                load_h1(c + 3)
+            if c >= 2:
+                finish_layernorm(c - 2)
+            if c < N_CHUNKS:
+                stage1(c)
+            if c == 0:
+                transposes(1)
+            if c + 2 < N_CHUNKS:
+                transposes(c + 2)
+            if 1 <= c <= N_CHUNKS:
+                centre_and_square(c - 1)
+            if c < N_CHUNKS:
+                u_tiles[c] = lnpool.tile([P, NI_TILES, CHUNK], F32, name="u_sb")
+                stage2_block(c, 0)
+            if 1 <= c <= N_CHUNKS:
+                inverse_std(c - 1)
+            if c < N_CHUNKS:
+                stage2_block(c, 1)

@@ -24,6 +24,7 @@ N_CHUNKS = BATCH // CHUNK
 M_TILES = H2 // P
 NI_TILES = NI // P
 LN_EPS = 1e-5
+VECTOR_BANKS = 1
 
 FLOPS = 2 * BATCH * H1 * H2 + 2 * BATCH * H2 * NI
 
@@ -197,9 +198,19 @@ def tile_capsulenetwork_pa_t_kernel(tc, h1, W2, b2, Wp, bp, ln_g, ln_b, out):
                             start=(g == 0),
                             stop=(g == PASSES - 1),
                         )
-                    nc.scalar.activation(
-                        out=x_rows[:, t, :], in_=acc[:], func=ACT.Relu, bias=b2_f[:, m : m + 1], scale=1.0
-                    )
+                    if m < VECTOR_BANKS:
+                        nc.vector.tensor_scalar(
+                            out=x_rows[:, t, :],
+                            in0=acc[:],
+                            scalar1=b2_f[:, m : m + 1],
+                            scalar2=0.0,
+                            op0=ALU.add,
+                            op1=ALU.max,
+                        )
+                    else:
+                        nc.scalar.activation(
+                            out=x_rows[:, t, :], in_=acc[:], func=ACT.Relu, bias=b2_f[:, m : m + 1], scale=1.0
+                        )
                 x_grp = xpool.tile([P, CHUNK, PACK], BF16, align_bytes=64)
                 nc.vector.tensor_copy(
                     out=x_grp[:].rearrange("p (c i) t -> p c t i", i=4),

@@ -24,7 +24,7 @@ N_CHUNKS = BATCH // CHUNK
 M_TILES = H2 // P
 NI_TILES = NI // P
 LN_EPS = 1e-5
-VECTOR_BANKS = 1
+GROUPS = 2 * CAPS
 
 FLOPS = 2 * BATCH * H1 * H2 + 2 * BATCH * H2 * NI
 
@@ -43,13 +43,9 @@ def tile_capsulenetwork_pa_t_kernel(tc, h1, W2, b2, Wp, bp, ln_g, ln_b, out):
         psum = ctx.enter_context(tc.psum_pool(name="psum", bufs=8))
         ctx.enter_context(tc.manual_schedule())
 
-        h_raw_tiles = {}
-        h_mx = {}
-        x_mx = {}
-        u_tiles = {}
-        centred = {}
-        sum_sq_tiles = {}
-        rstd_tiles = {}
+        h_raw_tiles, h_grp_tiles, h_mx = {}, {}, {}
+        x_rows_tiles, x_grp_tiles, x_mx = {}, {}, {}
+        u_tiles, centred, squares, sum_sq_tiles, rstd_tiles, y_tiles = {}, {}, {}, {}, {}, {}
 
         def load_h1(c):
             h_raw = hpool.tile([P, SUB * H1], BF16, name="h_raw")
@@ -103,9 +99,9 @@ def tile_capsulenetwork_pa_t_kernel(tc, h1, W2, b2, Wp, bp, ln_g, ln_b, out):
         nc.vector.tensor_reduce(
             out=in_group[:], in_=ident[:].rearrange("p (n i) -> p n i", i=CAP_DIM), axis=AXIS.X, op=ALU.add
         )
-        centre = consts.tile([P, P], F32)
+        centre_mat = consts.tile([P, P], F32)
         nc.vector.scalar_tensor_tensor(
-            out=centre[:].rearrange("p (n i) -> p n i", i=CAP_DIM),
+            out=centre_mat[:].rearrange("p (n i) -> p n i", i=CAP_DIM),
             in0=in_group[:].unsqueeze(2).to_broadcast([P, P // CAP_DIM, CAP_DIM]),
             scalar=-1.0 / CAP_DIM,
             in1=ident[:].rearrange("p (n i) -> p n i", i=CAP_DIM),
@@ -156,12 +152,11 @@ def tile_capsulenetwork_pa_t_kernel(tc, h1, W2, b2, Wp, bp, ln_g, ln_b, out):
                     in_=grouped[g][:].rearrange("p c t -> p (c t)"),
                 )
 
-        def transposes(c):
+        def transpose_h1(c):
             h_words = h_raw_tiles.pop(c)[:].bitcast(F32)
-            h_codes = hpool.tile([P, PASSES, CHUNK], U32, align_bytes=64)
-            h_scales = hpool.tile([P, PASSES, CHUNK], U8, align_bytes=64)
+            h_grp_tiles[c] = []
             for g in range(PASSES):
-                h_grp = hpool.tile([P, CHUNK * PACK], BF16, align_bytes=64)
+                h_grp = hpool.tile([P, CHUNK * PACK], BF16, align_bytes=64, name="h_grp")
                 h_grp_words = h_grp[:].bitcast(F32).rearrange("p (b u) -> p b u", u=2)
                 for hf in range(2):
                     tr = psum.tile([P, 2, 2 * P], F32, tag="bank")
@@ -174,158 +169,179 @@ def tile_capsulenetwork_pa_t_kernel(tc, h1, W2, b2, Wp, bp, ln_g, ln_b, out):
                     nc.scalar.copy(
                         out=h_grp_words[:, hf * 2 * P : (hf + 1) * 2 * P, :], in_=tr[:].rearrange("p u b -> p b u")
                     )
-                nc.vector.quantize_mx(
-                    out=h_codes[:, g, :].bitcast(FP8X4), scales=h_scales[:, g, :], in_=h_grp[:]
-                )
+                h_grp_tiles[c].append(h_grp)
+            h_codes = hpool.tile([P, PASSES, CHUNK], U32, align_bytes=64, name="h_codes")
+            h_scales = hpool.tile([P, PASSES, CHUNK], U8, align_bytes=64, name="h_scales")
             h_mx[c] = (h_codes, h_scales)
 
-        def stage1(c):
-            h_codes, h_scales = h_mx.pop(c)
-            x_codes = xpool.tile([P, PASSES, CHUNK], U32, align_bytes=64)
-            x_scales = xpool.tile([P, PASSES, CHUNK], U8, align_bytes=64)
-            for g2 in range(PASSES):
-                x_rows = xpool.tile([P, PACK, CHUNK], BF16)
-                for t in range(PACK):
-                    m = PACK * g2 + t
-                    acc = psum.tile([P, CHUNK], F32, tag="bank")
-                    for g in range(PASSES):
-                        nc.tensor.matmul_mx(
-                            out=acc[:],
-                            lhsT=w2_codes[:, g, m * P : (m + 1) * P].bitcast(FP8X4),
-                            lhsT_scale=w2_scales[:, g, m * P : (m + 1) * P],
-                            rhs=h_codes[:, g, :].bitcast(FP8X4),
-                            rhs_scale=h_scales[:, g, :],
-                            start=(g == 0),
-                            stop=(g == PASSES - 1),
-                        )
-                    if m < VECTOR_BANKS:
-                        nc.vector.tensor_scalar(
-                            out=x_rows[:, t, :],
-                            in0=acc[:],
-                            scalar1=b2_f[:, m : m + 1],
-                            scalar2=0.0,
-                            op0=ALU.add,
-                            op1=ALU.max,
-                        )
-                    else:
-                        nc.scalar.activation(
-                            out=x_rows[:, t, :], in_=acc[:], func=ACT.Relu, bias=b2_f[:, m : m + 1], scale=1.0
-                        )
-                x_grp = xpool.tile([P, CHUNK, PACK], BF16, align_bytes=64)
-                nc.vector.tensor_copy(
-                    out=x_grp[:].rearrange("p (c i) t -> p c t i", i=4),
-                    in_=x_rows[:].rearrange("p t (c i) -> p c t i", i=4),
-                )
-                nc.vector.quantize_mx(
-                    out=x_codes[:, g2, :].bitcast(FP8X4),
-                    scales=x_scales[:, g2, :],
-                    in_=x_grp[:].rearrange("p b t -> p (b t)"),
-                )
-            x_mx[c] = (x_codes, x_scales)
-
-        def stage2_block(c, j):
-            x_codes, x_scales = x_mx[c]
-            acc2 = psum.tile([P, CHUNK], F32, tag="bank")
-            for g2 in range(PASSES):
-                nc.tensor.matmul_mx(
-                    out=acc2[:],
-                    lhsT=wp_codes[:, g2, j * P : (j + 1) * P].bitcast(FP8X4),
-                    lhsT_scale=wp_scales[:, g2, j * P : (j + 1) * P],
-                    rhs=x_codes[:, g2, :].bitcast(FP8X4),
-                    rhs_scale=x_scales[:, g2, :],
-                    start=(g2 == 0),
-                    stop=(g2 == PASSES - 1),
-                )
-            nc.scalar.activation(
-                out=u_tiles[c][:, j, :], in_=acc2[:], func=ACT.Identity, bias=bp_f[:, j : j + 1], scale=1.0
+        def quantise_h1(c, g):
+            h_codes, h_scales = h_mx[c]
+            nc.vector.quantize_mx(
+                out=h_codes[:, g, :].bitcast(FP8X4), scales=h_scales[:, g, :], in_=h_grp_tiles[c][g][:]
             )
 
-        GROUPS = 2 * CAPS
-
-        def centre_and_square(c):
-            u_sb = u_tiles.pop(c)
-            sum_sq = lnpool.tile([P, 2 * GROUPS], F32)
-            centred[c] = []
-            for hf in range(2):
-                cb = psum.tile([P, 2, NI], F32, tag="bank")
-                for sl in range(2):
-                    s = 2 * hf + sl
-                    for j in range(NI_TILES):
-                        nc.tensor.matmul(
-                            out=cb[:, sl, j * P : (j + 1) * P],
-                            lhsT=u_sb[:, j, s * P : (s + 1) * P],
-                            rhs=centre[:],
-                            start=True,
-                            stop=True,
-                        )
-                sq = lnpool.tile([P, 2 * NI], F32)
-                nc.scalar.activation(out=sq[:], in_=cb[:].rearrange("p s f -> p (s f)"), func=ACT.Square)
-                nc.vector.tensor_reduce(
-                    out=sum_sq[:, hf * GROUPS : (hf + 1) * GROUPS],
-                    in_=sq[:].rearrange("p (n i) -> p n i", i=CAP_DIM),
-                    axis=AXIS.X,
-                    op=ALU.add,
+        def stage1(c, g2):
+            h_codes, h_scales = h_mx[c]
+            x_rows = xpool.tile([P, PACK, CHUNK], BF16, name="x_rows")
+            for t in range(PACK):
+                m = PACK * g2 + t
+                acc = psum.tile([P, CHUNK], F32, tag="bank")
+                for g in range(PASSES):
+                    nc.tensor.matmul_mx(
+                        out=acc[:],
+                        lhsT=w2_codes[:, g, m * P : (m + 1) * P].bitcast(FP8X4),
+                        lhsT_scale=w2_scales[:, g, m * P : (m + 1) * P],
+                        rhs=h_codes[:, g, :].bitcast(FP8X4),
+                        rhs_scale=h_scales[:, g, :],
+                        start=(g == 0),
+                        stop=(g == PASSES - 1),
+                    )
+                nc.scalar.activation(
+                    out=x_rows[:, t, :], in_=acc[:], func=ACT.Relu, bias=b2_f[:, m : m + 1], scale=1.0
                 )
-                centred[c].append(cb)
-            sum_sq_tiles[c] = sum_sq
+            x_rows_tiles[(c, g2)] = x_rows
+
+        def regroup_x(c, g2):
+            x_grp = xpool.tile([P, CHUNK, PACK], BF16, align_bytes=64, name="x_grp")
+            nc.vector.tensor_copy(
+                out=x_grp[:].rearrange("p (c i) t -> p c t i", i=4),
+                in_=x_rows_tiles.pop((c, g2))[:].rearrange("p t (c i) -> p c t i", i=4),
+            )
+            x_grp_tiles[(c, g2)] = x_grp
+
+        def quantise_x(c, g2):
+            if g2 == 0:
+                x_codes = xpool.tile([P, PASSES, CHUNK], U32, align_bytes=64, name="x_codes")
+                x_scales = xpool.tile([P, PASSES, CHUNK], U8, align_bytes=64, name="x_scales")
+                x_mx[c] = (x_codes, x_scales)
+            x_codes, x_scales = x_mx[c]
+            nc.vector.quantize_mx(
+                out=x_codes[:, g2, :].bitcast(FP8X4),
+                scales=x_scales[:, g2, :],
+                in_=x_grp_tiles.pop((c, g2))[:].rearrange("p b t -> p (b t)"),
+            )
+
+        def stage2(c):
+            x_codes, x_scales = x_mx.pop(c)
+            u_sb = lnpool.tile([P, NI_TILES, CHUNK], F32, name="u_sb")
+            for j in range(NI_TILES):
+                acc2 = psum.tile([P, CHUNK], F32, tag="bank")
+                for g2 in range(PASSES):
+                    nc.tensor.matmul_mx(
+                        out=acc2[:],
+                        lhsT=wp_codes[:, g2, j * P : (j + 1) * P].bitcast(FP8X4),
+                        lhsT_scale=wp_scales[:, g2, j * P : (j + 1) * P],
+                        rhs=x_codes[:, g2, :].bitcast(FP8X4),
+                        rhs_scale=x_scales[:, g2, :],
+                        start=(g2 == 0),
+                        stop=(g2 == PASSES - 1),
+                    )
+                nc.scalar.activation(
+                    out=u_sb[:, j, :], in_=acc2[:], func=ACT.Identity, bias=bp_f[:, j : j + 1], scale=1.0
+                )
+            u_tiles[c] = u_sb
+
+        def centre(c, hf):
+            u_sb = u_tiles[c]
+            cb = psum.tile([P, 2, NI], F32, tag="bank")
+            for sl in range(2):
+                s = 2 * hf + sl
+                for j in range(NI_TILES):
+                    nc.tensor.matmul(
+                        out=cb[:, sl, j * P : (j + 1) * P],
+                        lhsT=u_sb[:, j, s * P : (s + 1) * P],
+                        rhs=centre_mat[:],
+                        start=True,
+                        stop=True,
+                    )
+            sq = lnpool.tile([P, 2 * NI], F32, name="sq")
+            nc.scalar.activation(out=sq[:], in_=cb[:].rearrange("p s f -> p (s f)"), func=ACT.Square)
+            centred[(c, hf)] = cb
+            squares[(c, hf)] = sq
+
+        def sum_squares(c, hf):
+            if hf == 0:
+                sum_sq_tiles[c] = lnpool.tile([P, 2 * GROUPS], F32, name="sum_sq")
+            nc.vector.tensor_reduce(
+                out=sum_sq_tiles[c][:, hf * GROUPS : (hf + 1) * GROUPS],
+                in_=squares.pop((c, hf))[:].rearrange("p (n i) -> p n i", i=CAP_DIM),
+                axis=AXIS.X,
+                op=ALU.add,
+            )
 
         def inverse_std(c):
-            rstd = lnpool.tile([P, 2 * GROUPS], F32)
+            rstd = lnpool.tile([P, 2 * GROUPS], F32, name="rstd")
             nc.scalar.activation(
                 out=rstd[:], in_=sum_sq_tiles.pop(c)[:], func=ACT.Abs_reciprocal_sqrt, bias=eps[:], scale=1.0 / CAP_DIM
             )
             rstd_tiles[c] = rstd
 
-        def finish_layernorm(c):
-            rstd = rstd_tiles.pop(c)
-            banks = centred.pop(c)
-            y = lnpool.tile([P, SUB, NI], F32, bufs=3)
-            for hf in range(2):
-                nc.vector.tensor_tensor(
-                    out=y[:, 2 * hf : 2 * hf + 2, :].rearrange("p s (n i) -> p (s n) i", i=CAP_DIM),
-                    in0=banks[hf][:].rearrange("p s (n i) -> p (s n) i", i=CAP_DIM),
-                    in1=rstd[:, hf * GROUPS : (hf + 1) * GROUPS].unsqueeze(2).to_broadcast([P, GROUPS, CAP_DIM]),
-                    op=ALU.mult,
-                )
-            for hf in range(2):
-                nc.vector.tensor_tensor(
-                    out=y[:, 2 * hf : 2 * hf + 2, :],
-                    in0=y[:, 2 * hf : 2 * hf + 2, :],
-                    in1=gain[:].unsqueeze(1).to_broadcast([P, 2, NI]),
-                    op=ALU.mult,
-                )
-            for hf in range(2):
-                nc.vector.tensor_tensor(
-                    out=y[:, 2 * hf : 2 * hf + 2, :],
-                    in0=y[:, 2 * hf : 2 * hf + 2, :],
-                    in1=shift[:].unsqueeze(1).to_broadcast([P, 2, NI]),
-                    op=ALU.add,
-                )
-            nc.sync.dma_start(
-                out=out_rows[c * CHUNK : (c + 1) * CHUNK, :].rearrange("(p s) f -> p s f", s=SUB), in_=y[:]
+        def times_rstd(c, hf):
+            if hf == 0:
+                y_tiles[c] = lnpool.tile([P, SUB, NI], F32, name="y", bufs=3)
+            nc.vector.tensor_tensor(
+                out=y_tiles[c][:, 2 * hf : 2 * hf + 2, :].rearrange("p s (n i) -> p (s n) i", i=CAP_DIM),
+                in0=centred.pop((c, hf))[:].rearrange("p s (n i) -> p (s n) i", i=CAP_DIM),
+                in1=rstd_tiles[c][:, hf * GROUPS : (hf + 1) * GROUPS].unsqueeze(2).to_broadcast([P, GROUPS, CAP_DIM]),
+                op=ALU.mult,
             )
 
+        def affine(c, hf, table, op):
+            half = y_tiles[c][:, 2 * hf : 2 * hf + 2, :]
+            nc.vector.tensor_tensor(out=half, in0=half, in1=table[:].unsqueeze(1).to_broadcast([P, 2, NI]), op=op)
+
+        def store(c):
+            nc.sync.dma_start(
+                out=out_rows[c * CHUNK : (c + 1) * CHUNK, :].rearrange("(p s) f -> p s f", s=SUB), in_=y_tiles.pop(c)[:]
+            )
+
+        def exists(c):
+            return 0 <= c < N_CHUNKS
+
         quantise_w2(0)
-        transposes(0)
+        transpose_h1(0)
+        quantise_h1(0, 0)
+        quantise_h1(0, 1)
         quantise_w2(1)
         quantise_wp()
         for c in range(N_CHUNKS + 2):
-            if c + 3 < N_CHUNKS:
+            done, mid, ahead = c - 2, c - 1, c + 2
+            if exists(c + 3):
                 load_h1(c + 3)
-            if c >= 2:
-                finish_layernorm(c - 2)
-            if c < N_CHUNKS:
-                stage1(c)
+            if exists(done):
+                times_rstd(done, 0)
+                times_rstd(done, 1)
+                affine(done, 0, gain, ALU.mult)
+                affine(done, 1, gain, ALU.mult)
+                affine(done, 0, shift, ALU.add)
+            if exists(c):
+                stage1(c, 0)
+                regroup_x(c, 0)
+            if exists(done):
+                affine(done, 1, shift, ALU.add)
+                store(done)
+            if exists(c):
+                quantise_x(c, 0)
+                stage1(c, 1)
+                regroup_x(c, 1)
+            if exists(mid):
+                centre(mid, 0)
+                centre(mid, 1)
+                sum_squares(mid, 0)
+            if exists(c):
+                quantise_x(c, 1)
+            if exists(mid):
+                sum_squares(mid, 1)
             if c == 0:
-                transposes(1)
-            if c + 2 < N_CHUNKS:
-                transposes(c + 2)
-            if 1 <= c <= N_CHUNKS:
-                centre_and_square(c - 1)
-            if c < N_CHUNKS:
-                u_tiles[c] = lnpool.tile([P, NI_TILES, CHUNK], F32, name="u_sb")
-                stage2_block(c, 0)
-            if 1 <= c <= N_CHUNKS:
-                inverse_std(c - 1)
-            if c < N_CHUNKS:
-                stage2_block(c, 1)
+                transpose_h1(1)
+                quantise_h1(1, 0)
+                quantise_h1(1, 1)
+            if exists(ahead):
+                transpose_h1(ahead)
+            if exists(mid):
+                inverse_std(mid)
+            if exists(ahead):
+                quantise_h1(ahead, 0)
+                quantise_h1(ahead, 1)
+            if exists(c):
+                stage2(c)

@@ -26,6 +26,11 @@ NI_TILES = NI // P
 LN_EPS = 1e-5
 GROUPS = 2 * CAPS
 
+WORK_BANKS, CENTRED_BANKS = 6, 2
+SHIFT_ON_GPSIMD = True
+TAIL = (4,)
+SHIFT_ON_VECTOR_AT_END = 1
+
 FLOPS = 2 * BATCH * H1 * H2 + 2 * BATCH * H2 * NI
 
 
@@ -40,12 +45,22 @@ def tile_capsulenetwork_pa_t_kernel(tc, h1, W2, b2, Wp, bp, ln_g, ln_b, out):
         hpool = ctx.enter_context(tc.tile_pool(name="hpool", bufs=3))
         xpool = ctx.enter_context(tc.tile_pool(name="xpool", bufs=2))
         lnpool = ctx.enter_context(tc.tile_pool(name="lnpool", bufs=2))
-        psum = ctx.enter_context(tc.psum_pool(name="psum", bufs=8))
+        psum = ctx.enter_context(tc.psum_pool(name="psum", bufs=WORK_BANKS))
+        cent = ctx.enter_context(tc.psum_pool(name="cent", bufs=CENTRED_BANKS))
         ctx.enter_context(tc.manual_schedule())
 
         h_raw_tiles, h_grp_tiles, h_mx = {}, {}, {}
         x_rows_tiles, x_grp_tiles, x_mx = {}, {}, {}
         u_tiles, centred, squares, sum_sq_tiles, rstd_tiles, y_tiles = {}, {}, {}, {}, {}, {}
+
+        pieces = [(c, 0, SUB) for c in range(N_CHUNKS - 1)]
+        for ns in TAIL:
+            pieces.append((N_CHUNKS - 1, sum(p[2] for p in pieces if p[0] == N_CHUNKS - 1), ns))
+        N_PIECES = len(pieces)
+
+        def units(i):
+            ns = pieces[i][2]
+            return [(b, min(2, ns - b)) for b in range(0, ns, 2)]
 
         def load_h1(c):
             h_raw = hpool.tile([P, SUB * H1], BF16, name="h_raw")
@@ -154,10 +169,9 @@ def tile_capsulenetwork_pa_t_kernel(tc, h1, W2, b2, Wp, bp, ln_g, ln_b, out):
 
         def transpose_h1(c):
             h_words = h_raw_tiles.pop(c)[:].bitcast(F32)
-            h_grp_tiles[c] = []
+            h_grp = hpool.tile([P, PASSES, CHUNK * PACK], BF16, align_bytes=64, name="h_grp", bufs=2)
             for g in range(PASSES):
-                h_grp = hpool.tile([P, CHUNK * PACK], BF16, align_bytes=64, name="h_grp")
-                h_grp_words = h_grp[:].bitcast(F32).rearrange("p (b u) -> p b u", u=2)
+                h_grp_words = h_grp[:, g, :].bitcast(F32).rearrange("p (b u) -> p b u", u=2)
                 for hf in range(2):
                     tr = psum.tile([P, 2, 2 * P], F32, tag="bank")
                     for u in range(2):
@@ -169,179 +183,201 @@ def tile_capsulenetwork_pa_t_kernel(tc, h1, W2, b2, Wp, bp, ln_g, ln_b, out):
                     nc.scalar.copy(
                         out=h_grp_words[:, hf * 2 * P : (hf + 1) * 2 * P, :], in_=tr[:].rearrange("p u b -> p b u")
                     )
-                h_grp_tiles[c].append(h_grp)
+            h_grp_tiles[c] = h_grp
+
+        def quantise_h1(c):
             h_codes = hpool.tile([P, PASSES, CHUNK], U32, align_bytes=64, name="h_codes")
             h_scales = hpool.tile([P, PASSES, CHUNK], U8, align_bytes=64, name="h_scales")
             h_mx[c] = (h_codes, h_scales)
-
-        def quantise_h1(c, g):
-            h_codes, h_scales = h_mx[c]
             nc.vector.quantize_mx(
-                out=h_codes[:, g, :].bitcast(FP8X4), scales=h_scales[:, g, :], in_=h_grp_tiles[c][g][:]
+                out=h_codes[:].rearrange("p g b -> p (g b)").bitcast(FP8X4),
+                scales=h_scales[:].rearrange("p g b -> p (g b)"),
+                in_=h_grp_tiles.pop(c)[:].rearrange("p g n -> p (g n)"),
             )
 
-        def stage1(c, g2):
+        def stage1(i, g2):
+            c, s0, ns = pieces[i]
+            n = ns * P
+            cols = slice(s0 * P, s0 * P + n)
             h_codes, h_scales = h_mx[c]
-            x_rows = xpool.tile([P, PACK, CHUNK], BF16, name="x_rows")
+            x_rows = xpool.tile([P, PACK, CHUNK], BF16, name="x_rows", bufs=3)
             for t in range(PACK):
                 m = PACK * g2 + t
                 acc = psum.tile([P, CHUNK], F32, tag="bank")
                 for g in range(PASSES):
                     nc.tensor.matmul_mx(
-                        out=acc[:],
+                        out=acc[:, :n],
                         lhsT=w2_codes[:, g, m * P : (m + 1) * P].bitcast(FP8X4),
                         lhsT_scale=w2_scales[:, g, m * P : (m + 1) * P],
-                        rhs=h_codes[:, g, :].bitcast(FP8X4),
-                        rhs_scale=h_scales[:, g, :],
+                        rhs=h_codes[:, g, cols].bitcast(FP8X4),
+                        rhs_scale=h_scales[:, g, cols],
                         start=(g == 0),
                         stop=(g == PASSES - 1),
                     )
                 nc.scalar.activation(
-                    out=x_rows[:, t, :], in_=acc[:], func=ACT.Relu, bias=b2_f[:, m : m + 1], scale=1.0
+                    out=x_rows[:, t, :n], in_=acc[:, :n], func=ACT.Relu, bias=b2_f[:, m : m + 1], scale=1.0
                 )
-            x_rows_tiles[(c, g2)] = x_rows
+            x_rows_tiles[(i, g2)] = x_rows
 
-        def regroup_x(c, g2):
-            x_grp = xpool.tile([P, CHUNK, PACK], BF16, align_bytes=64, name="x_grp")
+        def regroup_x(i, g2):
+            n = pieces[i][2] * P
+            x_grp = xpool.tile([P, CHUNK, PACK], BF16, align_bytes=64, name="x_grp", bufs=3)
             nc.vector.tensor_copy(
-                out=x_grp[:].rearrange("p (c i) t -> p c t i", i=4),
-                in_=x_rows_tiles.pop((c, g2))[:].rearrange("p t (c i) -> p c t i", i=4),
+                out=x_grp[:, :n, :].rearrange("p (c i) t -> p c t i", i=4),
+                in_=x_rows_tiles.pop((i, g2))[:, :, :n].rearrange("p t (c i) -> p c t i", i=4),
             )
-            x_grp_tiles[(c, g2)] = x_grp
+            x_grp_tiles[(i, g2)] = x_grp
 
-        def quantise_x(c, g2):
+        def quantise_x(i, g2):
+            n = pieces[i][2] * P
             if g2 == 0:
                 x_codes = xpool.tile([P, PASSES, CHUNK], U32, align_bytes=64, name="x_codes")
                 x_scales = xpool.tile([P, PASSES, CHUNK], U8, align_bytes=64, name="x_scales")
-                x_mx[c] = (x_codes, x_scales)
-            x_codes, x_scales = x_mx[c]
+                x_mx[i] = (x_codes, x_scales)
+            x_codes, x_scales = x_mx[i]
             nc.vector.quantize_mx(
-                out=x_codes[:, g2, :].bitcast(FP8X4),
-                scales=x_scales[:, g2, :],
-                in_=x_grp_tiles.pop((c, g2))[:].rearrange("p b t -> p (b t)"),
+                out=x_codes[:, g2, :n].bitcast(FP8X4),
+                scales=x_scales[:, g2, :n],
+                in_=x_grp_tiles.pop((i, g2))[:, :n, :].rearrange("p b t -> p (b t)"),
             )
 
-        def stage2(c):
-            x_codes, x_scales = x_mx.pop(c)
+        def stage2(i):
+            n = pieces[i][2] * P
+            x_codes, x_scales = x_mx.pop(i)
             u_sb = lnpool.tile([P, NI_TILES, CHUNK], F32, name="u_sb")
             for j in range(NI_TILES):
                 acc2 = psum.tile([P, CHUNK], F32, tag="bank")
                 for g2 in range(PASSES):
                     nc.tensor.matmul_mx(
-                        out=acc2[:],
+                        out=acc2[:, :n],
                         lhsT=wp_codes[:, g2, j * P : (j + 1) * P].bitcast(FP8X4),
                         lhsT_scale=wp_scales[:, g2, j * P : (j + 1) * P],
-                        rhs=x_codes[:, g2, :].bitcast(FP8X4),
-                        rhs_scale=x_scales[:, g2, :],
+                        rhs=x_codes[:, g2, :n].bitcast(FP8X4),
+                        rhs_scale=x_scales[:, g2, :n],
                         start=(g2 == 0),
                         stop=(g2 == PASSES - 1),
                     )
                 nc.scalar.activation(
-                    out=u_sb[:, j, :], in_=acc2[:], func=ACT.Identity, bias=bp_f[:, j : j + 1], scale=1.0
+                    out=u_sb[:, j, :n], in_=acc2[:, :n], func=ACT.Identity, bias=bp_f[:, j : j + 1], scale=1.0
                 )
-            u_tiles[c] = u_sb
+            u_tiles[i] = u_sb
 
-        def centre(c, hf):
-            u_sb = u_tiles[c]
-            cb = psum.tile([P, 2, NI], F32, tag="bank")
-            for sl in range(2):
-                s = 2 * hf + sl
+        def centre(i, b0, nb):
+            u_sb = u_tiles[i]
+            cb = cent.tile([P, 2, NI], F32, tag="cent")
+            for sl in range(nb):
                 for j in range(NI_TILES):
                     nc.tensor.matmul(
                         out=cb[:, sl, j * P : (j + 1) * P],
-                        lhsT=u_sb[:, j, s * P : (s + 1) * P],
+                        lhsT=u_sb[:, j, (b0 + sl) * P : (b0 + sl + 1) * P],
                         rhs=centre_mat[:],
                         start=True,
                         stop=True,
                     )
             sq = lnpool.tile([P, 2 * NI], F32, name="sq")
-            nc.scalar.activation(out=sq[:], in_=cb[:].rearrange("p s f -> p (s f)"), func=ACT.Square)
-            centred[(c, hf)] = cb
-            squares[(c, hf)] = sq
+            nc.scalar.activation(
+                out=sq[:, : nb * NI], in_=cb[:, :nb, :].rearrange("p s f -> p (s f)"), func=ACT.Square
+            )
+            centred[(i, b0)] = cb
+            squares[(i, b0)] = sq
 
-        def sum_squares(c, hf):
-            if hf == 0:
-                sum_sq_tiles[c] = lnpool.tile([P, 2 * GROUPS], F32, name="sum_sq")
+        def times_gain(i, b0, nb):
+            if b0 == 0:
+                y_tiles[i] = lnpool.tile([P, SUB, NI], F32, name="y", bufs=4)
+            nc.vector.tensor_tensor(
+                out=y_tiles[i][:, b0 : b0 + nb, :],
+                in0=centred.pop((i, b0))[:, :nb, :],
+                in1=gain[:].unsqueeze(1).to_broadcast([P, nb, NI]),
+                op=ALU.mult,
+            )
+
+        def sum_squares(i, b0, nb):
+            if b0 == 0:
+                sum_sq_tiles[i] = lnpool.tile([P, SUB * CAPS], F32, name="sum_sq")
             nc.vector.tensor_reduce(
-                out=sum_sq_tiles[c][:, hf * GROUPS : (hf + 1) * GROUPS],
-                in_=squares.pop((c, hf))[:].rearrange("p (n i) -> p n i", i=CAP_DIM),
+                out=sum_sq_tiles[i][:, b0 * CAPS : (b0 + nb) * CAPS],
+                in_=squares.pop((i, b0))[:, : nb * NI].rearrange("p (n i) -> p n i", i=CAP_DIM),
                 axis=AXIS.X,
                 op=ALU.add,
             )
 
-        def inverse_std(c):
-            rstd = lnpool.tile([P, 2 * GROUPS], F32, name="rstd")
+        def inverse_std(i):
+            groups = pieces[i][2] * CAPS
+            rstd = lnpool.tile([P, SUB * CAPS], F32, name="rstd")
             nc.scalar.activation(
-                out=rstd[:], in_=sum_sq_tiles.pop(c)[:], func=ACT.Abs_reciprocal_sqrt, bias=eps[:], scale=1.0 / CAP_DIM
+                out=rstd[:, :groups],
+                in_=sum_sq_tiles.pop(i)[:, :groups],
+                func=ACT.Abs_reciprocal_sqrt,
+                bias=eps[:],
+                scale=1.0 / CAP_DIM,
             )
-            rstd_tiles[c] = rstd
+            rstd_tiles[i] = rstd
 
-        def times_rstd(c, hf):
-            if hf == 0:
-                y_tiles[c] = lnpool.tile([P, SUB, NI], F32, name="y", bufs=3)
+        def times_rstd(i):
+            ns = pieces[i][2]
+            y = y_tiles[i][:, :ns, :].rearrange("p s (n i) -> p (s n) i", i=CAP_DIM)
             nc.vector.tensor_tensor(
-                out=y_tiles[c][:, 2 * hf : 2 * hf + 2, :].rearrange("p s (n i) -> p (s n) i", i=CAP_DIM),
-                in0=centred.pop((c, hf))[:].rearrange("p s (n i) -> p (s n) i", i=CAP_DIM),
-                in1=rstd_tiles[c][:, hf * GROUPS : (hf + 1) * GROUPS].unsqueeze(2).to_broadcast([P, GROUPS, CAP_DIM]),
+                out=y,
+                in0=y,
+                in1=rstd_tiles.pop(i)[:, : ns * CAPS].unsqueeze(2).to_broadcast([P, ns * CAPS, CAP_DIM]),
                 op=ALU.mult,
             )
 
-        def affine(c, hf, table, op):
-            half = y_tiles[c][:, 2 * hf : 2 * hf + 2, :]
-            nc.vector.tensor_tensor(out=half, in0=half, in1=table[:].unsqueeze(1).to_broadcast([P, 2, NI]), op=op)
+        def plus_shift(i, b0, nb):
+            engine = nc.gpsimd if SHIFT_ON_GPSIMD and i < N_PIECES - SHIFT_ON_VECTOR_AT_END else nc.vector
+            part = y_tiles[i][:, b0 : b0 + nb, :]
+            engine.tensor_tensor(out=part, in0=part, in1=shift[:].unsqueeze(1).to_broadcast([P, nb, NI]), op=ALU.add)
 
-        def store(c):
+        def store(i):
+            c, s0, ns = pieces[i]
             nc.sync.dma_start(
-                out=out_rows[c * CHUNK : (c + 1) * CHUNK, :].rearrange("(p s) f -> p s f", s=SUB), in_=y_tiles.pop(c)[:]
+                out=out_rows[c * CHUNK : (c + 1) * CHUNK, :].rearrange("(p s) f -> p s f", s=SUB)[:, s0 : s0 + ns, :],
+                in_=y_tiles.pop(i)[:, :ns, :],
             )
 
-        def exists(c):
-            return 0 <= c < N_CHUNKS
+        def exists(i):
+            return 0 <= i < N_PIECES
 
         quantise_w2(0)
         transpose_h1(0)
-        quantise_h1(0, 0)
-        quantise_h1(0, 1)
+        quantise_h1(0)
         quantise_w2(1)
         quantise_wp()
-        for c in range(N_CHUNKS + 2):
-            done, mid, ahead = c - 2, c - 1, c + 2
-            if exists(c + 3):
+        for i in range(N_PIECES + 3):
+            opens = exists(i) and pieces[i][1] == 0
+            c = pieces[i][0] if exists(i) else N_CHUNKS
+            if opens and c + 3 < N_CHUNKS:
                 load_h1(c + 3)
-            if exists(done):
-                times_rstd(done, 0)
-                times_rstd(done, 1)
-                affine(done, 0, gain, ALU.mult)
-                affine(done, 1, gain, ALU.mult)
-                affine(done, 0, shift, ALU.add)
-            if exists(c):
-                stage1(c, 0)
-                regroup_x(c, 0)
-            if exists(done):
-                affine(done, 1, shift, ALU.add)
-                store(done)
-            if exists(c):
-                quantise_x(c, 0)
-                stage1(c, 1)
-                regroup_x(c, 1)
-            if exists(mid):
-                centre(mid, 0)
-                centre(mid, 1)
-                sum_squares(mid, 0)
-            if exists(c):
-                quantise_x(c, 1)
-            if exists(mid):
-                sum_squares(mid, 1)
-            if c == 0:
+            if exists(i - 2):
+                for b0, nb in units(i - 2):
+                    times_gain(i - 2, b0, nb)
+                    sum_squares(i - 2, b0, nb)
+            if exists(i - 3):
+                for b0, nb in units(i - 3):
+                    plus_shift(i - 3, b0, nb)
+                store(i - 3)
+            if exists(i):
+                stage1(i, 0)
+            if exists(i - 2):
+                inverse_std(i - 2)
+            if exists(i):
+                regroup_x(i, 0)
+                if opens and 0 < c and c + 1 < N_CHUNKS:
+                    quantise_h1(c + 1)
+                stage1(i, 1)
+                regroup_x(i, 1)
+                quantise_x(i, 0)
+                quantise_x(i, 1)
+            if opens and c == 0:
                 transpose_h1(1)
-                quantise_h1(1, 0)
-                quantise_h1(1, 1)
-            if exists(ahead):
-                transpose_h1(ahead)
-            if exists(mid):
-                inverse_std(mid)
-            if exists(ahead):
-                quantise_h1(ahead, 0)
-                quantise_h1(ahead, 1)
-            if exists(c):
-                stage2(c)
+            if opens and c + 2 < N_CHUNKS:
+                transpose_h1(c + 2)
+            if exists(i - 1):
+                for b0, nb in units(i - 1):
+                    centre(i - 1, b0, nb)
+            if opens and c == 0:
+                quantise_h1(1)
+            if exists(i - 2):
+                times_rstd(i - 2)
+            if exists(i):
+                stage2(i)

@@ -28,6 +28,8 @@ GROUPS = 2 * CAPS
 
 WORK_BANKS, CENTRED_BANKS = 6, 2
 SHIFT_ON_GPSIMD = True
+W2_ON_SCALAR = ((1, 0),)
+WP_ON_SCALAR = ()
 TAIL = (4,)
 SHIFT_ON_VECTOR_AT_END = 1
 
@@ -80,17 +82,29 @@ def tile_capsulenetwork_pa_t_kernel(tc, h1, W2, b2, Wp, bp, ln_g, ln_b, out):
 
         w2_raw = weights.tile([P, PASSES * PACK, H2], BF16)
 
-        def load_w2(half):
+        def load_w2(half, g):
             cols = slice(half * K_PASS, (half + 1) * K_PASS)
-            for a in range(PASSES * 2):
+            for a in (2 * g, 2 * g + 1):
                 nc.sync.dma_start(
                     out=w2_raw[:, 2 * a : 2 * a + 2, cols],
                     in_=W2[a * 256 : (a + 1) * 256, cols].rearrange("(q e) c -> q e c", e=2),
                 )
 
-        load_w2(0)
-        load_h1(0)
-        load_w2(1)
+        def load_h1_pass(c, g):
+            if g == 0:
+                h_raw_tiles[c] = hpool.tile([P, SUB * H1], BF16, name="h_raw")
+            ks = slice(g * K_PASS, (g + 1) * K_PASS)
+            nc.sync.dma_start(
+                out=h_raw_tiles[c][:].rearrange("p (s k) -> p s k", s=SUB)[:, :, ks],
+                in_=h1[c * CHUNK : (c + 1) * CHUNK, ks].rearrange("(p s) k -> p s k", s=SUB),
+            )
+
+        load_h1_pass(0, 0)
+        load_w2(0, 0)
+        load_h1_pass(0, 1)
+        load_w2(0, 1)
+        load_w2(1, 0)
+        load_w2(1, 1)
         load_h1(1)
         wp_raw = weights.tile([P, PASSES, CAPS, PACK * CAP_DIM], BF16)
         for g in range(PASSES):
@@ -131,46 +145,55 @@ def tile_capsulenetwork_pa_t_kernel(tc, h1, W2, b2, Wp, bp, ln_g, ln_b, out):
         w2_codes = weights.tile([P, PASSES, H2], U32, align_bytes=64)
         w2_scales = weights.tile([P, PASSES, H2], U8, align_bytes=64)
 
-        def quantise_w2(half):
+        w2_grp_tiles = {}
+
+        def regroup_w2(half, g):
             cols = slice(half * K_PASS, (half + 1) * K_PASS)
-            grouped = []
-            for g in range(PASSES):
-                w2_grp = wstage.tile([P, K_PASS, PACK], BF16, align_bytes=64)
-                nc.vector.tensor_copy(
-                    out=w2_grp[:].rearrange("p (t q) j -> p t q j", t=PACK),
-                    in_=w2_raw[:, PACK * g : PACK * (g + 1), cols].rearrange("p j (q t) -> p t q j", t=PACK),
-                )
-                grouped.append(w2_grp)
-            for g in range(PASSES):
-                nc.vector.quantize_mx(
-                    out=w2_codes[:, g, cols].bitcast(FP8X4),
-                    scales=w2_scales[:, g, cols],
-                    in_=grouped[g][:].rearrange("p c j -> p (c j)"),
-                )
+            w2_grp = wstage.tile([P, K_PASS, PACK], BF16, align_bytes=64, name="w2_grp", bufs=4)
+            dst = w2_grp[:].rearrange("p (t q) j -> p t q j", t=PACK)
+            src = w2_raw[:, PACK * g : PACK * (g + 1), cols].rearrange("p j (q t) -> p t q j", t=PACK)
+            if (half, g) in W2_ON_SCALAR:
+                nc.scalar.copy(out=dst, in_=src)
+            else:
+                nc.vector.tensor_copy(out=dst, in_=src)
+            w2_grp_tiles[(half, g)] = w2_grp
+
+        def quantise_w2(half, g):
+            cols = slice(half * K_PASS, (half + 1) * K_PASS)
+            nc.vector.quantize_mx(
+                out=w2_codes[:, g, cols].bitcast(FP8X4),
+                scales=w2_scales[:, g, cols],
+                in_=w2_grp_tiles.pop((half, g))[:].rearrange("p c j -> p (c j)"),
+            )
 
         wp_codes = weights.tile([P, PASSES, NI], U32, align_bytes=64)
         wp_scales = weights.tile([P, PASSES, NI], U8, align_bytes=64)
 
-        def quantise_wp():
-            grouped = []
-            for g in range(PASSES):
-                wp_grp = wstage.tile([P, NI, PACK], BF16, align_bytes=64)
-                nc.vector.tensor_copy(
-                    out=wp_grp[:].rearrange("p (n i) t -> p n i t", i=CAP_DIM),
-                    in_=wp_raw[:, g, :, :].rearrange("p n (t i) -> p n i t", t=PACK),
-                )
-                grouped.append(wp_grp)
-            for g in range(PASSES):
-                nc.vector.quantize_mx(
-                    out=wp_codes[:, g, :].bitcast(FP8X4),
-                    scales=wp_scales[:, g, :],
-                    in_=grouped[g][:].rearrange("p c t -> p (c t)"),
-                )
+        wp_grp_tiles = {}
 
-        def transpose_h1(c):
-            h_words = h_raw_tiles.pop(c)[:].bitcast(F32)
-            h_grp = hpool.tile([P, PASSES, CHUNK * PACK], BF16, align_bytes=64, name="h_grp", bufs=2)
-            for g in range(PASSES):
+        def regroup_wp(g):
+            wp_grp = wstage.tile([P, NI, PACK], BF16, align_bytes=64, name="wp_grp")
+            dst = wp_grp[:].rearrange("p (n i) t -> p n i t", i=CAP_DIM)
+            src = wp_raw[:, g, :, :].rearrange("p n (t i) -> p n i t", t=PACK)
+            if g in WP_ON_SCALAR:
+                nc.scalar.copy(out=dst, in_=src)
+            else:
+                nc.vector.tensor_copy(out=dst, in_=src)
+            wp_grp_tiles[g] = wp_grp
+
+        def quantise_wp(g):
+            nc.vector.quantize_mx(
+                out=wp_codes[:, g, :].bitcast(FP8X4),
+                scales=wp_scales[:, g, :],
+                in_=wp_grp_tiles.pop(g)[:].rearrange("p c t -> p (c t)"),
+            )
+
+        def transpose_h1(c, passes=(0, 1)):
+            h_words = h_raw_tiles[c][:].bitcast(F32)
+            if c not in h_grp_tiles:
+                h_grp_tiles[c] = hpool.tile([P, PASSES, CHUNK * PACK], BF16, align_bytes=64, name="h_grp", bufs=2)
+            h_grp = h_grp_tiles[c]
+            for g in passes:
                 h_grp_words = h_grp[:, g, :].bitcast(F32).rearrange("p (b u) -> p b u", u=2)
                 for hf in range(2):
                     tr = psum.tile([P, 2, 2 * P], F32, tag="bank")
@@ -183,39 +206,56 @@ def tile_capsulenetwork_pa_t_kernel(tc, h1, W2, b2, Wp, bp, ln_g, ln_b, out):
                     nc.scalar.copy(
                         out=h_grp_words[:, hf * 2 * P : (hf + 1) * 2 * P, :], in_=tr[:].rearrange("p u b -> p b u")
                     )
-            h_grp_tiles[c] = h_grp
 
-        def quantise_h1(c):
-            h_codes = hpool.tile([P, PASSES, CHUNK], U32, align_bytes=64, name="h_codes")
-            h_scales = hpool.tile([P, PASSES, CHUNK], U8, align_bytes=64, name="h_scales")
-            h_mx[c] = (h_codes, h_scales)
-            nc.vector.quantize_mx(
-                out=h_codes[:].rearrange("p g b -> p (g b)").bitcast(FP8X4),
-                scales=h_scales[:].rearrange("p g b -> p (g b)"),
-                in_=h_grp_tiles.pop(c)[:].rearrange("p g n -> p (g n)"),
-            )
+        def quantise_h1(c, g=None):
+            if c not in h_mx:
+                h_codes = hpool.tile([P, PASSES, CHUNK], U32, align_bytes=64, name="h_codes")
+                h_scales = hpool.tile([P, PASSES, CHUNK], U8, align_bytes=64, name="h_scales")
+                h_mx[c] = (h_codes, h_scales)
+            h_codes, h_scales = h_mx[c]
+            if g is None:
+                nc.vector.quantize_mx(
+                    out=h_codes[:].rearrange("p g b -> p (g b)").bitcast(FP8X4),
+                    scales=h_scales[:].rearrange("p g b -> p (g b)"),
+                    in_=h_grp_tiles[c][:].rearrange("p g n -> p (g n)"),
+                )
+            else:
+                nc.vector.quantize_mx(
+                    out=h_codes[:, g, :].bitcast(FP8X4), scales=h_scales[:, g, :], in_=h_grp_tiles[c][:, g, :]
+                )
 
-        def stage1(i, g2):
+        def stage1(i, g2, by_pass=False):
             c, s0, ns = pieces[i]
             n = ns * P
             cols = slice(s0 * P, s0 * P + n)
             h_codes, h_scales = h_mx[c]
             x_rows = xpool.tile([P, PACK, CHUNK], BF16, name="x_rows", bufs=3)
+            accs = {}
+
+            def one_pass(t, g):
+                m = PACK * g2 + t
+                if g == 0:
+                    accs[t] = psum.tile([P, CHUNK], F32, tag="bank", name="acc")
+                nc.tensor.matmul_mx(
+                    out=accs[t][:, :n],
+                    lhsT=w2_codes[:, g, m * P : (m + 1) * P].bitcast(FP8X4),
+                    lhsT_scale=w2_scales[:, g, m * P : (m + 1) * P],
+                    rhs=h_codes[:, g, cols].bitcast(FP8X4),
+                    rhs_scale=h_scales[:, g, cols],
+                    start=(g == 0),
+                    stop=(g == PASSES - 1),
+                )
+
+            if by_pass:
+                for t in range(PACK):
+                    one_pass(t, 0)
             for t in range(PACK):
                 m = PACK * g2 + t
-                acc = psum.tile([P, CHUNK], F32, tag="bank")
-                for g in range(PASSES):
-                    nc.tensor.matmul_mx(
-                        out=acc[:, :n],
-                        lhsT=w2_codes[:, g, m * P : (m + 1) * P].bitcast(FP8X4),
-                        lhsT_scale=w2_scales[:, g, m * P : (m + 1) * P],
-                        rhs=h_codes[:, g, cols].bitcast(FP8X4),
-                        rhs_scale=h_scales[:, g, cols],
-                        start=(g == 0),
-                        stop=(g == PASSES - 1),
-                    )
+                if not by_pass:
+                    one_pass(t, 0)
+                one_pass(t, 1)
                 nc.scalar.activation(
-                    out=x_rows[:, t, :n], in_=acc[:, :n], func=ACT.Relu, bias=b2_f[:, m : m + 1], scale=1.0
+                    out=x_rows[:, t, :n], in_=accs[t][:, :n], func=ACT.Relu, bias=b2_f[:, m : m + 1], scale=1.0
                 )
             x_rows_tiles[(i, g2)] = x_rows
 
@@ -338,12 +378,33 @@ def tile_capsulenetwork_pa_t_kernel(tc, h1, W2, b2, Wp, bp, ln_g, ln_b, out):
         def exists(i):
             return 0 <= i < N_PIECES
 
-        quantise_w2(0)
-        transpose_h1(0)
-        quantise_h1(0)
-        quantise_w2(1)
-        quantise_wp()
-        for i in range(N_PIECES + 3):
+        transpose_h1(0, (0,))
+        regroup_w2(0, 0)
+        quantise_h1(0, 0)
+        quantise_w2(0, 0)
+        transpose_h1(0, (1,))
+        regroup_w2(0, 1)
+        quantise_h1(0, 1)
+        quantise_w2(0, 1)
+        regroup_w2(1, 0)
+        regroup_w2(1, 1)
+        quantise_w2(1, 0)
+        quantise_w2(1, 1)
+        load_h1(3)
+        stage1(0, 0, by_pass=True)
+        transpose_h1(1)
+        regroup_x(0, 0)
+        regroup_wp(0)
+        stage1(0, 1)
+        quantise_h1(1)
+        regroup_wp(1)
+        quantise_wp(0)
+        transpose_h1(2)
+        regroup_x(0, 1)
+        quantise_wp(1)
+        quantise_x(0, 0)
+        quantise_x(0, 1)
+        for i in range(1, N_PIECES + 3):
             opens = exists(i) and pieces[i][1] == 0
             c = pieces[i][0] if exists(i) else N_CHUNKS
             if opens and c + 3 < N_CHUNKS:
@@ -365,18 +426,16 @@ def tile_capsulenetwork_pa_t_kernel(tc, h1, W2, b2, Wp, bp, ln_g, ln_b, out):
                 if opens and 0 < c and c + 1 < N_CHUNKS:
                     quantise_h1(c + 1)
                 stage1(i, 1)
+                if i == 1:
+                    stage2(0)
                 regroup_x(i, 1)
                 quantise_x(i, 0)
                 quantise_x(i, 1)
-            if opens and c == 0:
-                transpose_h1(1)
             if opens and c + 2 < N_CHUNKS:
                 transpose_h1(c + 2)
             if exists(i - 1):
                 for b0, nb in units(i - 1):
                     centre(i - 1, b0, nb)
-            if opens and c == 0:
-                quantise_h1(1)
             if exists(i - 2):
                 times_rstd(i - 2)
             if exists(i):

@@ -27,11 +27,13 @@ LN_EPS = 1e-5
 GROUPS = 2 * CAPS
 
 WORK_BANKS, CENTRED_BANKS = 6, 2
-SHIFT_ON_GPSIMD = True
 W2_ON_SCALAR = ((1, 0),)
-WP_ON_SCALAR = ()
-TAIL = (4,)
-SHIFT_ON_VECTOR_AT_END = 1
+RELU_ON_VECTOR_UNTIL = 3
+RELU_ON_VECTOR = ((0, 0),)
+UNITS = ((0, 2), (2, 2))
+LAST_UNITS = ((0, 2), (2, 1), (3, 1))
+HALVES = ((0, 2), (2, 2))
+WHOLE = (0, 4)
 
 FLOPS = 2 * BATCH * H1 * H2 + 2 * BATCH * H2 * NI
 
@@ -55,14 +57,6 @@ def tile_capsulenetwork_pa_t_kernel(tc, h1, W2, b2, Wp, bp, ln_g, ln_b, out):
         x_rows_tiles, x_grp_tiles, x_mx = {}, {}, {}
         u_tiles, centred, squares, sum_sq_tiles, rstd_tiles, y_tiles = {}, {}, {}, {}, {}, {}
 
-        pieces = [(c, 0, SUB) for c in range(N_CHUNKS - 1)]
-        for ns in TAIL:
-            pieces.append((N_CHUNKS - 1, sum(p[2] for p in pieces if p[0] == N_CHUNKS - 1), ns))
-        N_PIECES = len(pieces)
-
-        def units(i):
-            ns = pieces[i][2]
-            return [(b, min(2, ns - b)) for b in range(0, ns, 2)]
 
         def load_h1(c):
             h_raw = hpool.tile([P, SUB * H1], BF16, name="h_raw")
@@ -137,6 +131,7 @@ def tile_capsulenetwork_pa_t_kernel(tc, h1, W2, b2, Wp, bp, ln_g, ln_b, out):
             op0=ALU.mult,
             op1=ALU.add,
         )
+        centre_gain = consts.tile([P, NI_TILES, P], F32)
         b2_f = consts.tile([P, M_TILES], F32)
         nc.vector.tensor_copy(out=b2_f[:], in_=b2_bf[:].rearrange("p g t -> p (g t)"))
         bp_f = consts.tile([P, NI_TILES], F32)
@@ -175,10 +170,7 @@ def tile_capsulenetwork_pa_t_kernel(tc, h1, W2, b2, Wp, bp, ln_g, ln_b, out):
             wp_grp = wstage.tile([P, NI, PACK], BF16, align_bytes=64, name="wp_grp")
             dst = wp_grp[:].rearrange("p (n i) t -> p n i t", i=CAP_DIM)
             src = wp_raw[:, g, :, :].rearrange("p n (t i) -> p n i t", t=PACK)
-            if g in WP_ON_SCALAR:
-                nc.scalar.copy(out=dst, in_=src)
-            else:
-                nc.vector.tensor_copy(out=dst, in_=src)
+            nc.vector.tensor_copy(out=dst, in_=src)
             wp_grp_tiles[g] = wp_grp
 
         def quantise_wp(g):
@@ -187,6 +179,9 @@ def tile_capsulenetwork_pa_t_kernel(tc, h1, W2, b2, Wp, bp, ln_g, ln_b, out):
                 scales=wp_scales[:, g, :],
                 in_=wp_grp_tiles.pop(g)[:].rearrange("p c t -> p (c t)"),
             )
+
+        def columns(rng):
+            return slice(rng[0] * P, (rng[0] + rng[1]) * P)
 
         def transpose_h1(c, passes=(0, 1)):
             h_words = h_raw_tiles[c][:].bitcast(F32)
@@ -224,10 +219,7 @@ def tile_capsulenetwork_pa_t_kernel(tc, h1, W2, b2, Wp, bp, ln_g, ln_b, out):
                     out=h_codes[:, g, :].bitcast(FP8X4), scales=h_scales[:, g, :], in_=h_grp_tiles[c][:, g, :]
                 )
 
-        def stage1(i, g2, by_pass=False):
-            c, s0, ns = pieces[i]
-            n = ns * P
-            cols = slice(s0 * P, s0 * P + n)
+        def stage1(c, g2, by_pass=False):
             h_codes, h_scales = h_mx[c]
             x_rows = xpool.tile([P, PACK, CHUNK], BF16, name="x_rows", bufs=3)
             accs = {}
@@ -237,11 +229,11 @@ def tile_capsulenetwork_pa_t_kernel(tc, h1, W2, b2, Wp, bp, ln_g, ln_b, out):
                 if g == 0:
                     accs[t] = psum.tile([P, CHUNK], F32, tag="bank", name="acc")
                 nc.tensor.matmul_mx(
-                    out=accs[t][:, :n],
+                    out=accs[t][:],
                     lhsT=w2_codes[:, g, m * P : (m + 1) * P].bitcast(FP8X4),
                     lhsT_scale=w2_scales[:, g, m * P : (m + 1) * P],
-                    rhs=h_codes[:, g, cols].bitcast(FP8X4),
-                    rhs_scale=h_scales[:, g, cols],
+                    rhs=h_codes[:, g, :].bitcast(FP8X4),
+                    rhs_scale=h_scales[:, g, :],
                     start=(g == 0),
                     stop=(g == PASSES - 1),
                 )
@@ -254,37 +246,46 @@ def tile_capsulenetwork_pa_t_kernel(tc, h1, W2, b2, Wp, bp, ln_g, ln_b, out):
                 if not by_pass:
                     one_pass(t, 0)
                 one_pass(t, 1)
-                nc.scalar.activation(
-                    out=x_rows[:, t, :n], in_=accs[t][:, :n], func=ACT.Relu, bias=b2_f[:, m : m + 1], scale=1.0
-                )
-            x_rows_tiles[(i, g2)] = x_rows
+                if (g2, t) in RELU_ON_VECTOR and c < RELU_ON_VECTOR_UNTIL:
+                    nc.vector.tensor_scalar(
+                        out=x_rows[:, t, :],
+                        in0=accs[t][:],
+                        scalar1=b2_f[:, m : m + 1],
+                        scalar2=0.0,
+                        op0=ALU.add,
+                        op1=ALU.max,
+                    )
+                else:
+                    nc.scalar.activation(
+                        out=x_rows[:, t, :], in_=accs[t][:], func=ACT.Relu, bias=b2_f[:, m : m + 1], scale=1.0
+                    )
+            x_rows_tiles[(c, g2)] = x_rows
 
-        def regroup_x(i, g2):
-            n = pieces[i][2] * P
-            x_grp = xpool.tile([P, CHUNK, PACK], BF16, align_bytes=64, name="x_grp", bufs=3)
+        def regroup_x(c, g2, rng=WHOLE):
+            if (c, g2) not in x_grp_tiles:
+                x_grp_tiles[(c, g2)] = xpool.tile([P, CHUNK, PACK], BF16, align_bytes=64, name="x_grp", bufs=3)
             nc.vector.tensor_copy(
-                out=x_grp[:, :n, :].rearrange("p (c i) t -> p c t i", i=4),
-                in_=x_rows_tiles.pop((i, g2))[:, :, :n].rearrange("p t (c i) -> p c t i", i=4),
+                out=x_grp_tiles[(c, g2)][:, columns(rng), :].rearrange("p (c i) t -> p c t i", i=4),
+                in_=x_rows_tiles[(c, g2)][:, :, columns(rng)].rearrange("p t (c i) -> p c t i", i=4),
             )
-            x_grp_tiles[(i, g2)] = x_grp
 
-        def quantise_x(i, g2):
-            n = pieces[i][2] * P
-            if g2 == 0:
+        def quantise_x(c, g2, rng=WHOLE):
+            if c not in x_mx:
                 x_codes = xpool.tile([P, PASSES, CHUNK], U32, align_bytes=64, name="x_codes")
                 x_scales = xpool.tile([P, PASSES, CHUNK], U8, align_bytes=64, name="x_scales")
-                x_mx[i] = (x_codes, x_scales)
-            x_codes, x_scales = x_mx[i]
+                x_mx[c] = (x_codes, x_scales)
+            x_codes, x_scales = x_mx[c]
             nc.vector.quantize_mx(
-                out=x_codes[:, g2, :n].bitcast(FP8X4),
-                scales=x_scales[:, g2, :n],
-                in_=x_grp_tiles.pop((i, g2))[:, :n, :].rearrange("p b t -> p (b t)"),
+                out=x_codes[:, g2, columns(rng)].bitcast(FP8X4),
+                scales=x_scales[:, g2, columns(rng)],
+                in_=x_grp_tiles[(c, g2)][:, columns(rng), :].rearrange("p b t -> p (b t)"),
             )
 
-        def stage2(i):
-            n = pieces[i][2] * P
-            x_codes, x_scales = x_mx.pop(i)
-            u_sb = lnpool.tile([P, NI_TILES, CHUNK], F32, name="u_sb")
+        def stage2(c, rng=WHOLE):
+            n = rng[1] * P
+            x_codes, x_scales = x_mx[c]
+            if c not in u_tiles:
+                u_tiles[c] = lnpool.tile([P, NI_TILES, CHUNK], F32, name="u_sb")
             for j in range(NI_TILES):
                 acc2 = psum.tile([P, CHUNK], F32, tag="bank")
                 for g2 in range(PASSES):
@@ -292,92 +293,111 @@ def tile_capsulenetwork_pa_t_kernel(tc, h1, W2, b2, Wp, bp, ln_g, ln_b, out):
                         out=acc2[:, :n],
                         lhsT=wp_codes[:, g2, j * P : (j + 1) * P].bitcast(FP8X4),
                         lhsT_scale=wp_scales[:, g2, j * P : (j + 1) * P],
-                        rhs=x_codes[:, g2, :n].bitcast(FP8X4),
-                        rhs_scale=x_scales[:, g2, :n],
+                        rhs=x_codes[:, g2, columns(rng)].bitcast(FP8X4),
+                        rhs_scale=x_scales[:, g2, columns(rng)],
                         start=(g2 == 0),
                         stop=(g2 == PASSES - 1),
                     )
                 nc.scalar.activation(
-                    out=u_sb[:, j, :n], in_=acc2[:, :n], func=ACT.Identity, bias=bp_f[:, j : j + 1], scale=1.0
+                    out=u_tiles[c][:, j, columns(rng)],
+                    in_=acc2[:, :n],
+                    func=ACT.Identity,
+                    bias=bp_f[:, j : j + 1],
+                    scale=1.0,
                 )
-            u_tiles[i] = u_sb
 
-        def centre(i, b0, nb):
-            u_sb = u_tiles[i]
-            cb = cent.tile([P, 2, NI], F32, tag="cent")
-            for sl in range(nb):
+        def to_rows(c, rng, bank, matrix):
+            for sl in range(rng[1]):
                 for j in range(NI_TILES):
                     nc.tensor.matmul(
-                        out=cb[:, sl, j * P : (j + 1) * P],
-                        lhsT=u_sb[:, j, (b0 + sl) * P : (b0 + sl + 1) * P],
-                        rhs=centre_mat[:],
+                        out=bank[:, sl, j * P : (j + 1) * P],
+                        lhsT=u_tiles[c][:, j, (rng[0] + sl) * P : (rng[0] + sl + 1) * P],
+                        rhs=matrix(j),
                         start=True,
                         stop=True,
                     )
-            sq = lnpool.tile([P, 2 * NI], F32, name="sq")
-            nc.scalar.activation(
-                out=sq[:, : nb * NI], in_=cb[:, :nb, :].rearrange("p s f -> p (s f)"), func=ACT.Square
-            )
-            centred[(i, b0)] = cb
-            squares[(i, b0)] = sq
 
-        def times_gain(i, b0, nb):
-            if b0 == 0:
-                y_tiles[i] = lnpool.tile([P, SUB, NI], F32, name="y", bufs=4)
+        def centre(c, rng, pool=None):
+            if pool is None:
+                cb = cent.tile([P, 2, NI], F32, tag="cent")
+            else:
+                cb = pool.tile([P, 2, NI], F32, tag="bank")
+            to_rows(c, rng, cb, lambda j: centre_mat[:])
+            sq = lnpool.tile([P, 2 * NI], F32, name="sq", bufs=3)
+            nc.scalar.activation(
+                out=sq[:, : rng[1] * NI], in_=cb[:, : rng[1], :].rearrange("p s f -> p (s f)"), func=ACT.Square
+            )
+            centred[(c, rng)] = cb
+            squares[(c, rng)] = sq
+
+        def centre_with_gain(c, rng):
+            cg = psum.tile([P, 2, NI], F32, tag="bank", name="cg")
+            to_rows(c, rng, cg, lambda j: centre_gain[:, j, :])
+            with_gain[(c, rng)] = cg
+
+        def y_of(c, rng):
+            if c not in y_tiles:
+                y_tiles[c] = lnpool.tile([P, SUB, NI], F32, name="y", bufs=4)
+            return y_tiles[c][:, rng[0] : rng[0] + rng[1], :]
+
+        def times_gain(c, rng):
             nc.vector.tensor_tensor(
-                out=y_tiles[i][:, b0 : b0 + nb, :],
-                in0=centred.pop((i, b0))[:, :nb, :],
-                in1=gain[:].unsqueeze(1).to_broadcast([P, nb, NI]),
+                out=y_of(c, rng),
+                in0=centred.pop((c, rng))[:, : rng[1], :],
+                in1=gain[:].unsqueeze(1).to_broadcast([P, rng[1], NI]),
                 op=ALU.mult,
             )
 
-        def sum_squares(i, b0, nb):
-            if b0 == 0:
-                sum_sq_tiles[i] = lnpool.tile([P, SUB * CAPS], F32, name="sum_sq")
+        def groups(rng):
+            return slice(rng[0] * CAPS, (rng[0] + rng[1]) * CAPS)
+
+        def sum_squares(c, rng):
+            if c not in sum_sq_tiles:
+                sum_sq_tiles[c] = lnpool.tile([P, SUB * CAPS], F32, name="sum_sq")
             nc.vector.tensor_reduce(
-                out=sum_sq_tiles[i][:, b0 * CAPS : (b0 + nb) * CAPS],
-                in_=squares.pop((i, b0))[:, : nb * NI].rearrange("p (n i) -> p n i", i=CAP_DIM),
+                out=sum_sq_tiles[c][:, groups(rng)],
+                in_=squares.pop((c, rng))[:, : rng[1] * NI].rearrange("p (n i) -> p n i", i=CAP_DIM),
                 axis=AXIS.X,
                 op=ALU.add,
             )
 
-        def inverse_std(i):
-            groups = pieces[i][2] * CAPS
-            rstd = lnpool.tile([P, SUB * CAPS], F32, name="rstd")
+        def inverse_std(c, rng=WHOLE):
+            if c not in rstd_tiles:
+                rstd_tiles[c] = lnpool.tile([P, SUB * CAPS], F32, name="rstd")
             nc.scalar.activation(
-                out=rstd[:, :groups],
-                in_=sum_sq_tiles.pop(i)[:, :groups],
+                out=rstd_tiles[c][:, groups(rng)],
+                in_=sum_sq_tiles[c][:, groups(rng)],
                 func=ACT.Abs_reciprocal_sqrt,
                 bias=eps[:],
                 scale=1.0 / CAP_DIM,
             )
-            rstd_tiles[i] = rstd
 
-        def times_rstd(i):
-            ns = pieces[i][2]
-            y = y_tiles[i][:, :ns, :].rearrange("p s (n i) -> p (s n) i", i=CAP_DIM)
+        def times_rstd(c, rng=WHOLE):
+            y = y_of(c, rng).rearrange("p s (n i) -> p (s n) i", i=CAP_DIM)
+            src = y
+            if (c, rng) in with_gain:
+                src = with_gain.pop((c, rng))[:, : rng[1], :].rearrange("p s (n i) -> p (s n) i", i=CAP_DIM)
             nc.vector.tensor_tensor(
                 out=y,
-                in0=y,
-                in1=rstd_tiles.pop(i)[:, : ns * CAPS].unsqueeze(2).to_broadcast([P, ns * CAPS, CAP_DIM]),
+                in0=src,
+                in1=rstd_tiles[c][:, groups(rng)].unsqueeze(2).to_broadcast([P, rng[1] * CAPS, CAP_DIM]),
                 op=ALU.mult,
             )
 
-        def plus_shift(i, b0, nb):
-            engine = nc.gpsimd if SHIFT_ON_GPSIMD and i < N_PIECES - SHIFT_ON_VECTOR_AT_END else nc.vector
-            part = y_tiles[i][:, b0 : b0 + nb, :]
-            engine.tensor_tensor(out=part, in0=part, in1=shift[:].unsqueeze(1).to_broadcast([P, nb, NI]), op=ALU.add)
-
-        def store(i):
-            c, s0, ns = pieces[i]
-            nc.sync.dma_start(
-                out=out_rows[c * CHUNK : (c + 1) * CHUNK, :].rearrange("(p s) f -> p s f", s=SUB)[:, s0 : s0 + ns, :],
-                in_=y_tiles.pop(i)[:, :ns, :],
+        def plus_shift(c, rng, engine):
+            engine.tensor_tensor(
+                out=y_of(c, rng), in0=y_of(c, rng), in1=shift[:].unsqueeze(1).to_broadcast([P, rng[1], NI]), op=ALU.add
             )
 
-        def exists(i):
-            return 0 <= i < N_PIECES
+        def store(c, rng=WHOLE):
+            nc.sync.dma_start(
+                out=out_rows[c * CHUNK : (c + 1) * CHUNK, :].rearrange("(p s) f -> p s f", s=SUB)[
+                    :, rng[0] : rng[0] + rng[1], :
+                ],
+                in_=y_of(c, rng),
+            )
 
+        with_gain = {}
         transpose_h1(0, (0,))
         regroup_w2(0, 0)
         quantise_h1(0, 0)
@@ -404,39 +424,79 @@ def tile_capsulenetwork_pa_t_kernel(tc, h1, W2, b2, Wp, bp, ln_g, ln_b, out):
         quantise_wp(1)
         quantise_x(0, 0)
         quantise_x(0, 1)
-        for i in range(1, N_PIECES + 3):
-            opens = exists(i) and pieces[i][1] == 0
-            c = pieces[i][0] if exists(i) else N_CHUNKS
-            if opens and c + 3 < N_CHUNKS:
+        quantise_h1(2)
+        LAST = N_CHUNKS - 1
+        for c in range(1, N_CHUNKS):
+            if c + 3 < N_CHUNKS:
                 load_h1(c + 3)
-            if exists(i - 2):
-                for b0, nb in units(i - 2):
-                    times_gain(i - 2, b0, nb)
-                    sum_squares(i - 2, b0, nb)
-            if exists(i - 3):
-                for b0, nb in units(i - 3):
-                    plus_shift(i - 3, b0, nb)
-                store(i - 3)
-            if exists(i):
-                stage1(i, 0)
-            if exists(i - 2):
-                inverse_std(i - 2)
-            if exists(i):
-                regroup_x(i, 0)
-                if opens and 0 < c and c + 1 < N_CHUNKS:
-                    quantise_h1(c + 1)
-                stage1(i, 1)
-                if i == 1:
-                    stage2(0)
-                regroup_x(i, 1)
-                quantise_x(i, 0)
-                quantise_x(i, 1)
-            if opens and c + 2 < N_CHUNKS:
+            if c == 2:
+                nc.vector.tensor_tensor(
+                    out=centre_gain[:],
+                    in0=centre_mat[:].unsqueeze(1).to_broadcast([P, NI_TILES, P]),
+                    in1=gain[:].rearrange("p (j f) -> p j f", j=NI_TILES),
+                    op=ALU.mult,
+                )
+            if c >= 2:
+                for unit in UNITS:
+                    times_gain(c - 2, unit)
+                    sum_squares(c - 2, unit)
+            if c >= 3:
+                for unit in UNITS:
+                    plus_shift(c - 3, unit, nc.gpsimd)
+                store(c - 3)
+            stage1(c, 0)
+            if c == LAST:
+                stage2(c - 1)
+            regroup_x(c, 0)
+            quantise_x(c, 0)
+            stage1(c, 1)
+            if c == 1:
+                stage2(0)
+            if c >= 2:
+                inverse_std(c - 2)
+            if c < LAST:
+                regroup_x(c, 1)
+                quantise_x(c, 1)
+            else:
+                for half in HALVES:
+                    regroup_x(c, 1, half)
+                for half in HALVES:
+                    quantise_x(c, 1, half)
+            if c + 2 < N_CHUNKS:
                 transpose_h1(c + 2)
-            if exists(i - 1):
-                for b0, nb in units(i - 1):
-                    centre(i - 1, b0, nb)
-            if exists(i - 2):
-                times_rstd(i - 2)
-            if exists(i):
-                stage2(i)
+            for unit in UNITS:
+                centre(c - 1, unit)
+            if c == LAST:
+                centre_with_gain(c - 1, UNITS[0])
+            if c + 2 < N_CHUNKS:
+                quantise_h1(c + 2)
+            if c >= 2:
+                times_rstd(c - 2)
+            if c < LAST - 1:
+                stage2(c)
+        for half in HALVES:
+            stage2(LAST, half)
+        sum_squares(LAST - 1, UNITS[0])
+        times_gain(LAST - 1, UNITS[1])
+        sum_squares(LAST - 1, UNITS[1])
+        for unit in UNITS:
+            plus_shift(LAST - 2, unit, nc.gpsimd)
+        store(LAST - 2)
+        inverse_std(LAST - 1)
+        for unit in LAST_UNITS:
+            centre(LAST, unit, psum)
+        for unit in UNITS:
+            times_rstd(LAST - 1, unit)
+        for unit in UNITS:
+            plus_shift(LAST - 1, unit, nc.gpsimd)
+        store(LAST - 1)
+        for unit in LAST_UNITS:
+            times_gain(LAST, unit)
+            sum_squares(LAST, unit)
+            inverse_std(LAST, unit)
+        times_rstd(LAST, LAST_UNITS[0])
+        for k in range(len(LAST_UNITS)):
+            if k + 1 < len(LAST_UNITS):
+                times_rstd(LAST, LAST_UNITS[k + 1])
+            plus_shift(LAST, LAST_UNITS[k], nc.vector)
+            store(LAST, LAST_UNITS[k])

@@ -485,13 +485,14 @@ def tile_capsulenetwork_pa_t_kernel(tc, h1, W2, b2, Wp, bp, ln_g, ln_b, out):
         inverse_std(LAST - 1)
         for unit in LAST_UNITS:
             centre(LAST, unit, psum)
+        for unit in LAST_UNITS:
+            centre_with_gain(LAST, unit)
         for unit in UNITS:
             times_rstd(LAST - 1, unit)
         for unit in UNITS:
             plus_shift(LAST - 1, unit, nc.gpsimd)
         store(LAST - 1)
         for unit in LAST_UNITS:
-            times_gain(LAST, unit)
             sum_squares(LAST, unit)
             inverse_std(LAST, unit)
         times_rstd(LAST, LAST_UNITS[0])

@@ -137,8 +137,8 @@ def tile_capsulenetwork_pa_t_kernel(tc, h1, W2, b2, Wp, bp, ln_g, ln_b, out):
         bp_f = consts.tile([P, NI_TILES], F32)
         nc.vector.tensor_copy(out=bp_f[:], in_=bp_bf[:])
 
-        w2_codes = weights.tile([P, PASSES, H2], U32, align_bytes=64)
-        w2_scales = weights.tile([P, PASSES, H2], U8, align_bytes=64)
+        w2_codes = weights.tile([P, PASSES, H2], U32, align_bytes=256)
+        w2_scales = weights.tile([P, PASSES, H2], U8, align_bytes=256)
 
         w2_grp_tiles = {}
 
@@ -161,8 +161,8 @@ def tile_capsulenetwork_pa_t_kernel(tc, h1, W2, b2, Wp, bp, ln_g, ln_b, out):
                 in_=w2_grp_tiles.pop((half, g))[:].rearrange("p c j -> p (c j)"),
             )
 
-        wp_codes = weights.tile([P, PASSES, NI], U32, align_bytes=64)
-        wp_scales = weights.tile([P, PASSES, NI], U8, align_bytes=64)
+        wp_codes = weights.tile([P, PASSES, NI], U32, align_bytes=256)
+        wp_scales = weights.tile([P, PASSES, NI], U8, align_bytes=256)
 
         wp_grp_tiles = {}
 
@@ -204,8 +204,8 @@ def tile_capsulenetwork_pa_t_kernel(tc, h1, W2, b2, Wp, bp, ln_g, ln_b, out):
 
         def quantise_h1(c, g=None):
             if c not in h_mx:
-                h_codes = hpool.tile([P, PASSES, CHUNK], U32, align_bytes=64, name="h_codes")
-                h_scales = hpool.tile([P, PASSES, CHUNK], U8, align_bytes=64, name="h_scales")
+                h_codes = hpool.tile([P, PASSES, CHUNK], U32, align_bytes=256, name="h_codes")
+                h_scales = hpool.tile([P, PASSES, CHUNK], U8, align_bytes=256, name="h_scales")
                 h_mx[c] = (h_codes, h_scales)
             h_codes, h_scales = h_mx[c]
             if g is None:
@@ -271,8 +271,8 @@ def tile_capsulenetwork_pa_t_kernel(tc, h1, W2, b2, Wp, bp, ln_g, ln_b, out):
 
         def quantise_x(c, g2, rng=WHOLE):
             if c not in x_mx:
-                x_codes = xpool.tile([P, PASSES, CHUNK], U32, align_bytes=64, name="x_codes")
-                x_scales = xpool.tile([P, PASSES, CHUNK], U8, align_bytes=64, name="x_scales")
+                x_codes = xpool.tile([P, PASSES, CHUNK], U32, align_bytes=256, name="x_codes")
+                x_scales = xpool.tile([P, PASSES, CHUNK], U8, align_bytes=256, name="x_scales")
                 x_mx[c] = (x_codes, x_scales)
             x_codes, x_scales = x_mx[c]
             nc.vector.quantize_mx(

@@ -27,7 +27,7 @@ LN_EPS = 1e-5
 GROUPS = 2 * CAPS
 
 WORK_BANKS, CENTRED_BANKS = 6, 2
-W2_ON_SCALAR = ((1, 0),)
+W2_ON_SCALAR = {(0, 0): 32, (0, 1): 32, (1, 0): 96, (1, 1): 0}
 RELU_ON_VECTOR_UNTIL = 3
 RELU_ON_VECTOR = ((0, 0),)
 UNITS = ((0, 2), (2, 2))
@@ -147,10 +147,10 @@ def tile_capsulenetwork_pa_t_kernel(tc, h1, W2, b2, Wp, bp, ln_g, ln_b, out):
             w2_grp = wstage.tile([P, K_PASS, PACK], BF16, align_bytes=64, name="w2_grp", bufs=4)
             dst = w2_grp[:].rearrange("p (t q) j -> p t q j", t=PACK)
             src = w2_raw[:, PACK * g : PACK * (g + 1), cols].rearrange("p j (q t) -> p t q j", t=PACK)
-            if (half, g) in W2_ON_SCALAR:
-                nc.scalar.copy(out=dst, in_=src)
-            else:
-                nc.vector.tensor_copy(out=dst, in_=src)
+            n = W2_ON_SCALAR[(half, g)]
+            nc.vector.tensor_copy(out=dst[:, :, n:, :], in_=src[:, :, n:, :])
+            if n:
+                nc.scalar.copy(out=dst[:, :, :n, :], in_=src[:, :, :n, :])
             w2_grp_tiles[(half, g)] = w2_grp
 
         def quantise_w2(half, g):
@@ -261,10 +261,10 @@ def tile_capsulenetwork_pa_t_kernel(tc, h1, W2, b2, Wp, bp, ln_g, ln_b, out):
                     )
             x_rows_tiles[(c, g2)] = x_rows
 
-        def regroup_x(c, g2, rng=WHOLE):
+        def regroup_x(c, g2, rng=WHOLE, copy=nc.vector.tensor_copy):
             if (c, g2) not in x_grp_tiles:
                 x_grp_tiles[(c, g2)] = xpool.tile([P, CHUNK, PACK], BF16, align_bytes=64, name="x_grp", bufs=3)
-            nc.vector.tensor_copy(
+            copy(
                 out=x_grp_tiles[(c, g2)][:, columns(rng), :].rearrange("p (c i) t -> p c t i", i=4),
                 in_=x_rows_tiles[(c, g2)][:, :, columns(rng)].rearrange("p t (c i) -> p c t i", i=4),
             )
@@ -323,12 +323,14 @@ def tile_capsulenetwork_pa_t_kernel(tc, h1, W2, b2, Wp, bp, ln_g, ln_b, out):
             else:
                 cb = pool.tile([P, 2, NI], F32, tag="bank")
             to_rows(c, rng, cb, lambda j: centre_mat[:])
-            sq = lnpool.tile([P, 2 * NI], F32, name="sq", bufs=3)
+            if c not in squares:
+                squares[c] = lnpool.tile([P, SUB, NI], F32, name="sq", bufs=3)
             nc.scalar.activation(
-                out=sq[:, : rng[1] * NI], in_=cb[:, : rng[1], :].rearrange("p s f -> p (s f)"), func=ACT.Square
+                out=squares[c][:, rng[0] : rng[0] + rng[1], :].rearrange("p s f -> p (s f)"),
+                in_=cb[:, : rng[1], :].rearrange("p s f -> p (s f)"),
+                func=ACT.Square,
             )
             centred[(c, rng)] = cb
-            squares[(c, rng)] = sq
 
         def centre_with_gain(c, rng):
             cg = psum.tile([P, 2, NI], F32, tag="bank", name="cg")
@@ -351,12 +353,12 @@ def tile_capsulenetwork_pa_t_kernel(tc, h1, W2, b2, Wp, bp, ln_g, ln_b, out):
         def groups(rng):
             return slice(rng[0] * CAPS, (rng[0] + rng[1]) * CAPS)
 
-        def sum_squares(c, rng):
+        def sum_squares(c, rng=WHOLE):
             if c not in sum_sq_tiles:
                 sum_sq_tiles[c] = lnpool.tile([P, SUB * CAPS], F32, name="sum_sq")
             nc.vector.tensor_reduce(
                 out=sum_sq_tiles[c][:, groups(rng)],
-                in_=squares.pop((c, rng))[:, : rng[1] * NI].rearrange("p (n i) -> p n i", i=CAP_DIM),
+                in_=squares[c][:, rng[0] : rng[0] + rng[1], :].rearrange("p s (n i) -> p (s n) i", i=CAP_DIM),
                 axis=AXIS.X,
                 op=ALU.add,
             )
@@ -439,7 +441,7 @@ def tile_capsulenetwork_pa_t_kernel(tc, h1, W2, b2, Wp, bp, ln_g, ln_b, out):
             if c >= 2:
                 for unit in UNITS:
                     times_gain(c - 2, unit)
-                    sum_squares(c - 2, unit)
+                sum_squares(c - 2)
             if c >= 3:
                 for unit in UNITS:
                     plus_shift(c - 3, unit, nc.gpsimd)
@@ -458,8 +460,8 @@ def tile_capsulenetwork_pa_t_kernel(tc, h1, W2, b2, Wp, bp, ln_g, ln_b, out):
                 regroup_x(c, 1)
                 quantise_x(c, 1)
             else:
-                for half in HALVES:
-                    regroup_x(c, 1, half)
+                regroup_x(c, 1, HALVES[0])
+                regroup_x(c, 1, HALVES[1], nc.scalar.copy)
                 for half in HALVES:
                     quantise_x(c, 1, half)
             if c + 2 < N_CHUNKS:
@@ -474,30 +476,35 @@ def tile_capsulenetwork_pa_t_kernel(tc, h1, W2, b2, Wp, bp, ln_g, ln_b, out):
                 times_rstd(c - 2)
             if c < LAST - 1:
                 stage2(c)
-        for half in HALVES:
-            stage2(LAST, half)
         sum_squares(LAST - 1, UNITS[0])
-        times_gain(LAST - 1, UNITS[1])
         sum_squares(LAST - 1, UNITS[1])
-        for unit in UNITS:
-            plus_shift(LAST - 2, unit, nc.gpsimd)
-        store(LAST - 2)
+        stage2(LAST, HALVES[0])
         inverse_std(LAST - 1)
-        for unit in LAST_UNITS:
-            centre(LAST, unit, psum)
-        for unit in LAST_UNITS:
-            centre_with_gain(LAST, unit)
+        stage2(LAST, HALVES[1])
+        times_gain(LAST - 1, UNITS[1])
         for unit in UNITS:
             times_rstd(LAST - 1, unit)
         for unit in UNITS:
-            plus_shift(LAST - 1, unit, nc.gpsimd)
-        store(LAST - 1)
+            plus_shift(LAST - 2, unit, nc.gpsimd)
+        store(LAST - 2)
+        for unit in LAST_UNITS:
+            centre(LAST, unit, psum)
+        for unit in LAST_UNITS[:0:-1]:
+            centre_with_gain(LAST, unit)
+        times_gain(LAST, LAST_UNITS[0])
         for unit in LAST_UNITS:
             sum_squares(LAST, unit)
+        for unit in LAST_UNITS[:2]:
             inverse_std(LAST, unit)
-        times_rstd(LAST, LAST_UNITS[0])
-        for k in range(len(LAST_UNITS)):
-            if k + 1 < len(LAST_UNITS):
-                times_rstd(LAST, LAST_UNITS[k + 1])
-            plus_shift(LAST, LAST_UNITS[k], nc.vector)
-            store(LAST, LAST_UNITS[k])
+            times_rstd(LAST, unit)
+        for unit in UNITS:
+            plus_shift(LAST - 1, unit, nc.gpsimd)
+        store(LAST - 1)
+        inverse_std(LAST, LAST_UNITS[2])
+        plus_shift(LAST, LAST_UNITS[0], nc.vector)
+        store(LAST, LAST_UNITS[0])
+        times_rstd(LAST, LAST_UNITS[2])
+        plus_shift(LAST, LAST_UNITS[1], nc.gpsimd)
+        store(LAST, LAST_UNITS[1])
+        plus_shift(LAST, LAST_UNITS[2], nc.vector)
+        store(LAST, LAST_UNITS[2])

@@ -26,7 +26,7 @@ NI_TILES = NI // P
 LN_EPS = 1e-5
 GROUPS = 2 * CAPS
 
-WORK_BANKS, CENTRED_BANKS = 6, 2
+BANKS = 8
 W2_ON_SCALAR = {(0, 0): 32, (0, 1): 32, (1, 0): 96, (1, 1): 0}
 RELU_ON_VECTOR_UNTIL = 3
 RELU_ON_VECTOR = ((0, 0),)
@@ -49,8 +49,7 @@ def tile_capsulenetwork_pa_t_kernel(tc, h1, W2, b2, Wp, bp, ln_g, ln_b, out):
         hpool = ctx.enter_context(tc.tile_pool(name="hpool", bufs=3))
         xpool = ctx.enter_context(tc.tile_pool(name="xpool", bufs=2))
         lnpool = ctx.enter_context(tc.tile_pool(name="lnpool", bufs=2))
-        psum = ctx.enter_context(tc.psum_pool(name="psum", bufs=WORK_BANKS))
-        cent = ctx.enter_context(tc.psum_pool(name="cent", bufs=CENTRED_BANKS))
+        psum = ctx.enter_context(tc.psum_pool(name="psum", bufs=BANKS))
         ctx.enter_context(tc.manual_schedule())
 
         h_raw_tiles, h_grp_tiles, h_mx = {}, {}, {}
@@ -319,7 +318,7 @@ def tile_capsulenetwork_pa_t_kernel(tc, h1, W2, b2, Wp, bp, ln_g, ln_b, out):
 
         def centre(c, rng, pool=None):
             if pool is None:
-                cb = cent.tile([P, 2, NI], F32, tag="cent")
+                cb = psum.tile([P, 2, NI], F32, tag="bank")
             else:
                 cb = pool.tile([P, 2, NI], F32, tag="bank")
             to_rows(c, rng, cb, lambda j: centre_mat[:])

from contextlib import ExitStack

import concourse.mybir as mybir
from concourse.masks import make_identity

F32 = mybir.dt.float32
BF16 = mybir.dt.bfloat16
U32 = mybir.dt.uint32
U8 = mybir.dt.uint8
FP8X4 = mybir.dt.float8_e4m3fn_x4
ALU = mybir.AluOpType
ACT = mybir.ActivationFunctionType
AXIS = mybir.AxisListType

P = 128
PACK = 4
K_PASS = P * PACK
BATCH, H1, H2, CAPS, CAP_DIM = 4096, 1024, 1024, 32, 8
NI = CAPS * CAP_DIM
PASSES = H1 // K_PASS
CHUNK = 512
SUB = CHUNK // P
N_CHUNKS = BATCH // CHUNK
M_TILES = H2 // P
NI_TILES = NI // P
LN_EPS = 1e-5
GROUPS = 2 * CAPS

BANKS = 8
W2_ON_SCALAR = {(0, 0): 32, (0, 1): 32, (1, 0): 96, (1, 1): 0}
RELU_ON_VECTOR_UNTIL = 3
RELU_ON_VECTOR = ((0, 0),)
UNITS = ((0, 2), (2, 2))
LAST_UNITS = ((0, 2), (2, 1), (3, 1))
HALVES = ((0, 2), (2, 2))
WHOLE = (0, 4)

FLOPS = 2 * BATCH * H1 * H2 + 2 * BATCH * H2 * NI


def tile_capsulenetwork_pa_t_kernel(tc, h1, W2, b2, Wp, bp, ln_g, ln_b, out):
    nc = tc.nc
    out_rows = out.rearrange("b n i -> b (n i)")

    with ExitStack() as ctx:
        consts = ctx.enter_context(tc.tile_pool(name="consts", bufs=1))
        weights = ctx.enter_context(tc.tile_pool(name="weights", bufs=1))
        wstage = ctx.enter_context(tc.tile_pool(name="wstage", bufs=2))
        hpool = ctx.enter_context(tc.tile_pool(name="hpool", bufs=3))
        xpool = ctx.enter_context(tc.tile_pool(name="xpool", bufs=2))
        lnpool = ctx.enter_context(tc.tile_pool(name="lnpool", bufs=2))
        psum = ctx.enter_context(tc.psum_pool(name="psum", bufs=BANKS))
        ctx.enter_context(tc.manual_schedule())

        h_raw_tiles, h_grp_tiles, h_mx = {}, {}, {}
        x_rows_tiles, x_grp_tiles, x_mx = {}, {}, {}
        u_tiles, centred, squares, sum_sq_tiles, rstd_tiles, y_tiles = {}, {}, {}, {}, {}, {}


        def load_h1(c):
            h_raw = hpool.tile([P, SUB * H1], BF16, name="h_raw")
            nc.sync.dma_start(
                out=h_raw[:],
                in_=h1[c * CHUNK : (c + 1) * CHUNK, :].rearrange("(p s) k -> p (s k)", s=SUB),
            )
            h_raw_tiles[c] = h_raw

        b2_bf = consts.tile([P, PASSES, PACK], BF16)
        nc.scalar.dma_start(out=b2_bf[:], in_=b2.rearrange("(g p t) -> p g t", g=PASSES, t=PACK))
        bp_bf = consts.tile([P, NI_TILES], BF16)
        with nc.allow_non_contiguous_dma(reason="256 bias values, one to a partition"):
            nc.scalar.dma_start(
                out=bp_bf[:], in_=bp.rearrange("n i -> (n i)").rearrange("(j q) -> q j", j=NI_TILES)
            )

        w2_raw = weights.tile([P, PASSES * PACK, H2], BF16)

        def load_w2(half, g):
            cols = slice(half * K_PASS, (half + 1) * K_PASS)
            for a in (2 * g, 2 * g + 1):
                nc.sync.dma_start(
                    out=w2_raw[:, 2 * a : 2 * a + 2, cols],
                    in_=W2[a * 256 : (a + 1) * 256, cols].rearrange("(q e) c -> q e c", e=2),
                )

        def load_h1_pass(c, g):
            if g == 0:
                h_raw_tiles[c] = hpool.tile([P, SUB * H1], BF16, name="h_raw")
            ks = slice(g * K_PASS, (g + 1) * K_PASS)
            nc.sync.dma_start(
                out=h_raw_tiles[c][:].rearrange("p (s k) -> p s k", s=SUB)[:, :, ks],
                in_=h1[c * CHUNK : (c + 1) * CHUNK, ks].rearrange("(p s) k -> p s k", s=SUB),
            )

        load_h1_pass(0, 0)
        load_w2(0, 0)
        load_h1_pass(0, 1)
        load_w2(0, 1)
        load_w2(1, 0)
        load_w2(1, 1)
        load_h1(1)
        wp_raw = weights.tile([P, PASSES, CAPS, PACK * CAP_DIM], BF16)
        for g in range(PASSES):
            nc.sync.dma_start(
                out=wp_raw[:, g, :, :],
                in_=Wp[:, g * K_PASS : (g + 1) * K_PASS, :].rearrange("n (p t) i -> p n (t i)", t=PACK),
            )
        load_h1(2)
        gain = consts.tile([P, NI], BF16)
        nc.sync.dma_start(out=gain[:], in_=ln_g.rearrange("n i -> (n i)").partition_broadcast(P))
        shift = consts.tile([P, NI], BF16)
        nc.sync.dma_start(out=shift[:], in_=ln_b.rearrange("n i -> (n i)").partition_broadcast(P))

        eps = consts.tile([P, 1], F32)
        nc.vector.memset(eps[:], LN_EPS)
        warm = consts.tile([P, 1], F32)
        nc.scalar.activation(out=warm[:], in_=eps[:], func=ACT.Abs_reciprocal_sqrt)
        ident = consts.tile([P, P], F32)
        make_identity(nc, ident[:])
        in_group = consts.tile([P, P // CAP_DIM], F32)
        nc.vector.tensor_reduce(
            out=in_group[:], in_=ident[:].rearrange("p (n i) -> p n i", i=CAP_DIM), axis=AXIS.X, op=ALU.add
        )
        centre_mat = consts.tile([P, P], F32)
        nc.vector.scalar_tensor_tensor(
            out=centre_mat[:].rearrange("p (n i) -> p n i", i=CAP_DIM),
            in0=in_group[:].unsqueeze(2).to_broadcast([P, P // CAP_DIM, CAP_DIM]),
            scalar=-1.0 / CAP_DIM,
            in1=ident[:].rearrange("p (n i) -> p n i", i=CAP_DIM),
            op0=ALU.mult,
            op1=ALU.add,
        )
        centre_gain = consts.tile([P, NI_TILES, P], F32)
        b2_f = consts.tile([P, M_TILES], F32)
        nc.vector.tensor_copy(out=b2_f[:], in_=b2_bf[:].rearrange("p g t -> p (g t)"))
        bp_f = consts.tile([P, NI_TILES], F32)
        nc.vector.tensor_copy(out=bp_f[:], in_=bp_bf[:])

        w2_codes = weights.tile([P, PASSES, H2], U32, align_bytes=256)
        w2_scales = weights.tile([P, PASSES, H2], U8, align_bytes=256)

        w2_grp_tiles = {}

        def regroup_w2(half, g):
            cols = slice(half * K_PASS, (half + 1) * K_PASS)
            w2_grp = wstage.tile([P, K_PASS, PACK], BF16, align_bytes=64, name="w2_grp", bufs=4)
            dst = w2_grp[:].rearrange("p (t q) j -> p t q j", t=PACK)
            src = w2_raw[:, PACK * g : PACK * (g + 1), cols].rearrange("p j (q t) -> p t q j", t=PACK)
            n = W2_ON_SCALAR[(half, g)]
            nc.vector.tensor_copy(out=dst[:, :, n:, :], in_=src[:, :, n:, :])
            if n:
                nc.scalar.copy(out=dst[:, :, :n, :], in_=src[:, :, :n, :])
            w2_grp_tiles[(half, g)] = w2_grp

        def quantise_w2(half, g):
            cols = slice(half * K_PASS, (half + 1) * K_PASS)
            nc.vector.quantize_mx(
                out=w2_codes[:, g, cols].bitcast(FP8X4),
                scales=w2_scales[:, g, cols],
                in_=w2_grp_tiles.pop((half, g))[:].rearrange("p c j -> p (c j)"),
            )

        wp_codes = weights.tile([P, PASSES, NI], U32, align_bytes=256)
        wp_scales = weights.tile([P, PASSES, NI], U8, align_bytes=256)

        wp_grp_tiles = {}

        def regroup_wp(g):
            wp_grp = wstage.tile([P, NI, PACK], BF16, align_bytes=64, name="wp_grp")
            dst = wp_grp[:].rearrange("p (n i) t -> p n i t", i=CAP_DIM)
            src = wp_raw[:, g, :, :].rearrange("p n (t i) -> p n i t", t=PACK)
            nc.vector.tensor_copy(out=dst, in_=src)
            wp_grp_tiles[g] = wp_grp

        def quantise_wp(g):
            nc.vector.quantize_mx(
                out=wp_codes[:, g, :].bitcast(FP8X4),
                scales=wp_scales[:, g, :],
                in_=wp_grp_tiles.pop(g)[:].rearrange("p c t -> p (c t)"),
            )

        def columns(rng):
            return slice(rng[0] * P, (rng[0] + rng[1]) * P)

        def transpose_h1(c, passes=(0, 1)):
            h_words = h_raw_tiles[c][:].bitcast(F32)
            if c not in h_grp_tiles:
                h_grp_tiles[c] = hpool.tile([P, PASSES, CHUNK * PACK], BF16, align_bytes=64, name="h_grp", bufs=2)
            h_grp = h_grp_tiles[c]
            for g in passes:
                h_grp_words = h_grp[:, g, :].bitcast(F32).rearrange("p (b u) -> p b u", u=2)
                for hf in range(2):
                    tr = psum.tile([P, 2, 2 * P], F32, tag="bank")
                    for u in range(2):
                        for sl in range(2):
                            first = (2 * hf + sl) * (H1 // 2) + 256 * g + P * u
                            nc.tensor.transpose(
                                tr[:, u, sl * P : (sl + 1) * P], h_words[:, first : first + P], ident[:]
                            )
                    nc.scalar.copy(
                        out=h_grp_words[:, hf * 2 * P : (hf + 1) * 2 * P, :], in_=tr[:].rearrange("p u b -> p b u")
                    )

        def quantise_h1(c, g=None):
            if c not in h_mx:
                h_codes = hpool.tile([P, PASSES, CHUNK], U32, align_bytes=256, name="h_codes")
                h_scales = hpool.tile([P, PASSES, CHUNK], U8, align_bytes=256, name="h_scales")
                h_mx[c] = (h_codes, h_scales)
            h_codes, h_scales = h_mx[c]
            if g is None:
                nc.vector.quantize_mx(
                    out=h_codes[:].rearrange("p g b -> p (g b)").bitcast(FP8X4),
                    scales=h_scales[:].rearrange("p g b -> p (g b)"),
                    in_=h_grp_tiles[c][:].rearrange("p g n -> p (g n)"),
                )
            else:
                nc.vector.quantize_mx(
                    out=h_codes[:, g, :].bitcast(FP8X4), scales=h_scales[:, g, :], in_=h_grp_tiles[c][:, g, :]
                )

        def stage1(c, g2, by_pass=False):
            h_codes, h_scales = h_mx[c]
            x_rows = xpool.tile([P, PACK, CHUNK], BF16, name="x_rows", bufs=3)
            accs = {}

            def one_pass(t, g):
                m = PACK * g2 + t
                if g == 0:
                    accs[t] = psum.tile([P, CHUNK], F32, tag="bank", name="acc")
                nc.tensor.matmul_mx(
                    out=accs[t][:],
                    lhsT=w2_codes[:, g, m * P : (m + 1) * P].bitcast(FP8X4),
                    lhsT_scale=w2_scales[:, g, m * P : (m + 1) * P],
                    rhs=h_codes[:, g, :].bitcast(FP8X4),
                    rhs_scale=h_scales[:, g, :],
                    start=(g == 0),
                    stop=(g == PASSES - 1),
                )

            if by_pass:
                for t in range(PACK):
                    one_pass(t, 0)
            for t in range(PACK):
                m = PACK * g2 + t
                if not by_pass:
                    one_pass(t, 0)
                one_pass(t, 1)
                if (g2, t) in RELU_ON_VECTOR and c < RELU_ON_VECTOR_UNTIL:
                    nc.vector.tensor_scalar(
                        out=x_rows[:, t, :],
                        in0=accs[t][:],
                        scalar1=b2_f[:, m : m + 1],
                        scalar2=0.0,
                        op0=ALU.add,
                        op1=ALU.max,
                    )
                else:
                    nc.scalar.activation(
                        out=x_rows[:, t, :], in_=accs[t][:], func=ACT.Relu, bias=b2_f[:, m : m + 1], scale=1.0
                    )
            x_rows_tiles[(c, g2)] = x_rows

        def regroup_x(c, g2, rng=WHOLE, copy=nc.vector.tensor_copy):
            if (c, g2) not in x_grp_tiles:
                x_grp_tiles[(c, g2)] = xpool.tile([P, CHUNK, PACK], BF16, align_bytes=64, name="x_grp", bufs=3)
            copy(
                out=x_grp_tiles[(c, g2)][:, columns(rng), :].rearrange("p (c i) t -> p c t i", i=4),
                in_=x_rows_tiles[(c, g2)][:, :, columns(rng)].rearrange("p t (c i) -> p c t i", i=4),
            )

        def quantise_x(c, g2, rng=WHOLE):
            if c not in x_mx:
                x_codes = xpool.tile([P, PASSES, CHUNK], U32, align_bytes=256, name="x_codes")
                x_scales = xpool.tile([P, PASSES, CHUNK], U8, align_bytes=256, name="x_scales")
                x_mx[c] = (x_codes, x_scales)
            x_codes, x_scales = x_mx[c]
            nc.vector.quantize_mx(
                out=x_codes[:, g2, columns(rng)].bitcast(FP8X4),
                scales=x_scales[:, g2, columns(rng)],
                in_=x_grp_tiles[(c, g2)][:, columns(rng), :].rearrange("p b t -> p (b t)"),
            )

        def stage2(c, rng=WHOLE):
            n = rng[1] * P
            x_codes, x_scales = x_mx[c]
            if c not in u_tiles:
                u_tiles[c] = lnpool.tile([P, NI_TILES, CHUNK], F32, name="u_sb")
            for j in range(NI_TILES):
                acc2 = psum.tile([P, CHUNK], F32, tag="bank")
                for g2 in range(PASSES):
                    nc.tensor.matmul_mx(
                        out=acc2[:, :n],
                        lhsT=wp_codes[:, g2, j * P : (j + 1) * P].bitcast(FP8X4),
                        lhsT_scale=wp_scales[:, g2, j * P : (j + 1) * P],
                        rhs=x_codes[:, g2, columns(rng)].bitcast(FP8X4),
                        rhs_scale=x_scales[:, g2, columns(rng)],
                        start=(g2 == 0),
                        stop=(g2 == PASSES - 1),
                    )
                nc.scalar.activation(
                    out=u_tiles[c][:, j, columns(rng)],
                    in_=acc2[:, :n],
                    func=ACT.Identity,
                    bias=bp_f[:, j : j + 1],
                    scale=1.0,
                )

        def to_rows(c, rng, bank, matrix):
            for sl in range(rng[1]):
                for j in range(NI_TILES):
                    nc.tensor.matmul(
                        out=bank[:, sl, j * P : (j + 1) * P],
                        lhsT=u_tiles[c][:, j, (rng[0] + sl) * P : (rng[0] + sl + 1) * P],
                        rhs=matrix(j),
                        start=True,
                        stop=True,
                    )

        def centre(c, rng, pool=None):
            if pool is None:
                cb = psum.tile([P, 2, NI], F32, tag="bank")
            else:
                cb = pool.tile([P, 2, NI], F32, tag="bank")
            to_rows(c, rng, cb, lambda j: centre_mat[:])
            if c not in squares:
                squares[c] = lnpool.tile([P, SUB, NI], F32, name="sq", bufs=3)
            nc.scalar.activation(
                out=squares[c][:, rng[0] : rng[0] + rng[1], :].rearrange("p s f -> p (s f)"),
                in_=cb[:, : rng[1], :].rearrange("p s f -> p (s f)"),
                func=ACT.Square,
            )
            centred[(c, rng)] = cb

        def centre_with_gain(c, rng):
            cg = psum.tile([P, 2, NI], F32, tag="bank", name="cg")
            to_rows(c, rng, cg, lambda j: centre_gain[:, j, :])
            with_gain[(c, rng)] = cg

        def y_of(c, rng):
            if c not in y_tiles:
                y_tiles[c] = lnpool.tile([P, SUB, NI], F32, name="y", bufs=4)
            return y_tiles[c][:, rng[0] : rng[0] + rng[1], :]

        def times_gain(c, rng):
            nc.vector.tensor_tensor(
                out=y_of(c, rng),
                in0=centred.pop((c, rng))[:, : rng[1], :],
                in1=gain[:].unsqueeze(1).to_broadcast([P, rng[1], NI]),
                op=ALU.mult,
            )

        def groups(rng):
            return slice(rng[0] * CAPS, (rng[0] + rng[1]) * CAPS)

        def sum_squares(c, rng=WHOLE):
            if c not in sum_sq_tiles:
                sum_sq_tiles[c] = lnpool.tile([P, SUB * CAPS], F32, name="sum_sq")
            nc.vector.tensor_reduce(
                out=sum_sq_tiles[c][:, groups(rng)],
                in_=squares[c][:, rng[0] : rng[0] + rng[1], :].rearrange("p s (n i) -> p (s n) i", i=CAP_DIM),
                axis=AXIS.X,
                op=ALU.add,
            )

        def inverse_std(c, rng=WHOLE):
            if c not in rstd_tiles:
                rstd_tiles[c] = lnpool.tile([P, SUB * CAPS], F32, name="rstd")
            nc.scalar.activation(
                out=rstd_tiles[c][:, groups(rng)],
                in_=sum_sq_tiles[c][:, groups(rng)],
                func=ACT.Abs_reciprocal_sqrt,
                bias=eps[:],
                scale=1.0 / CAP_DIM,
            )

        def times_rstd(c, rng=WHOLE):
            y = y_of(c, rng).rearrange("p s (n i) -> p (s n) i", i=CAP_DIM)
            src = y
            if (c, rng) in with_gain:
                src = with_gain.pop((c, rng))[:, : rng[1], :].rearrange("p s (n i) -> p (s n) i", i=CAP_DIM)
            nc.vector.tensor_tensor(
                out=y,
                in0=src,
                in1=rstd_tiles[c][:, groups(rng)].unsqueeze(2).to_broadcast([P, rng[1] * CAPS, CAP_DIM]),
                op=ALU.mult,
            )

        def plus_shift(c, rng, engine):
            engine.tensor_tensor(
                out=y_of(c, rng), in0=y_of(c, rng), in1=shift[:].unsqueeze(1).to_broadcast([P, rng[1], NI]), op=ALU.add
            )

        def store(c, rng=WHOLE):
            nc.sync.dma_start(
                out=out_rows[c * CHUNK : (c + 1) * CHUNK, :].rearrange("(p s) f -> p s f", s=SUB)[
                    :, rng[0] : rng[0] + rng[1], :
                ],
                in_=y_of(c, rng),
            )

        with_gain = {}
        transpose_h1(0, (0,))
        regroup_w2(0, 0)
        quantise_h1(0, 0)
        quantise_w2(0, 0)
        transpose_h1(0, (1,))
        regroup_w2(0, 1)
        quantise_h1(0, 1)
        quantise_w2(0, 1)
        regroup_w2(1, 0)
        regroup_w2(1, 1)
        quantise_w2(1, 0)
        quantise_w2(1, 1)
        load_h1(3)
        stage1(0, 0, by_pass=True)
        transpose_h1(1)
        regroup_x(0, 0)
        regroup_wp(0)
        stage1(0, 1)
        quantise_h1(1)
        regroup_wp(1)
        quantise_wp(0)
        transpose_h1(2)
        regroup_x(0, 1)
        quantise_wp(1)
        quantise_x(0, 0)
        quantise_x(0, 1)
        quantise_h1(2)
        LAST = N_CHUNKS - 1
        for c in range(1, N_CHUNKS):
            if c + 3 < N_CHUNKS:
                load_h1(c + 3)
            if c == 2:
                nc.vector.tensor_tensor(
                    out=centre_gain[:],
                    in0=centre_mat[:].unsqueeze(1).to_broadcast([P, NI_TILES, P]),
                    in1=gain[:].rearrange("p (j f) -> p j f", j=NI_TILES),
                    op=ALU.mult,
                )
            if c >= 2:
                for unit in UNITS:
                    times_gain(c - 2, unit)
                sum_squares(c - 2)
            if c >= 3:
                for unit in UNITS:
                    plus_shift(c - 3, unit, nc.gpsimd)
                store(c - 3)
            stage1(c, 0)
            if c == LAST:
                stage2(c - 1)
            regroup_x(c, 0)
            quantise_x(c, 0)
            stage1(c, 1)
            if c == 1:
                stage2(0)
            if c >= 2:
                inverse_std(c - 2)
            if c < LAST:
                regroup_x(c, 1)
                quantise_x(c, 1)
            else:
                regroup_x(c, 1, HALVES[0])
                regroup_x(c, 1, HALVES[1], nc.scalar.copy)
                for half in HALVES:
                    quantise_x(c, 1, half)
            if c + 2 < N_CHUNKS:
                transpose_h1(c + 2)
            for unit in UNITS:
                centre(c - 1, unit)
            if c == LAST:
                centre_with_gain(c - 1, UNITS[0])
            if c + 2 < N_CHUNKS:
                quantise_h1(c + 2)
            if c >= 2:
                times_rstd(c - 2)
            if c < LAST - 1:
                stage2(c)
        sum_squares(LAST - 1, UNITS[0])
        sum_squares(LAST - 1, UNITS[1])
        stage2(LAST, HALVES[0])
        inverse_std(LAST - 1)
        stage2(LAST, HALVES[1])
        times_gain(LAST - 1, UNITS[1])
        for unit in UNITS:
            times_rstd(LAST - 1, unit)
        for unit in UNITS:
            plus_shift(LAST - 2, unit, nc.gpsimd)
        store(LAST - 2)
        for unit in LAST_UNITS:
            centre(LAST, unit, psum)
        for unit in LAST_UNITS[:0:-1]:
            centre_with_gain(LAST, unit)
        times_gain(LAST, LAST_UNITS[0])
        for unit in LAST_UNITS:
            sum_squares(LAST, unit)
        for unit in LAST_UNITS[:2]:
            inverse_std(LAST, unit)
            times_rstd(LAST, unit)
        for unit in UNITS:
            plus_shift(LAST - 1, unit, nc.gpsimd)
        store(LAST - 1)
        inverse_std(LAST, LAST_UNITS[2])
        plus_shift(LAST, LAST_UNITS[0], nc.vector)
        store(LAST, LAST_UNITS[0])
        times_rstd(LAST, LAST_UNITS[2])
        plus_shift(LAST, LAST_UNITS[1], nc.gpsimd)
        store(LAST, LAST_UNITS[1])
        plus_shift(LAST, LAST_UNITS[2], nc.vector)
        store(LAST, LAST_UNITS[2])
